import numpy as np
import ml_dtypes


def mxq(x, axis, fmt="e4m3"):
    dtype, down = {"e4m3": (ml_dtypes.float8_e4m3fn, 7), "e5m2": (ml_dtypes.float8_e5m2, 14)}[fmt]
    v = np.moveaxis(np.asarray(x, np.float32).astype(ml_dtypes.bfloat16).astype(np.float64), axis, -1)
    blocks = v.reshape(v.shape[:-1] + (-1, 32))
    amax = np.abs(blocks).max(-1, keepdims=True)
    byte = np.maximum(np.where(amax > 0, np.frexp(amax)[1] - 1 + 127, 0) - down, 1)
    scale = np.exp2(byte - 127.0)
    codes = (blocks / scale).astype(np.float32).astype(dtype).astype(np.float64)
    return np.moveaxis((codes * scale).reshape(v.shape), -1, axis)


WIDE = False


def mx_kscale(k):
    if not WIDE:
        return np.ones(k)
    levels = np.array([10, -10, 5, -5, 0])
    a = np.random.permutation(np.resize(levels, k // 512 * 4)).reshape(k // 512, 4)
    idx = np.arange(k)
    return np.exp2(a[idx // 512, idx % 128 // 32])


BF16 = ml_dtypes.bfloat16


def bf(x):
    return np.asarray(x, np.float32).astype(BF16)


def f64(x):
    return np.asarray(x).astype(np.float64)


B, T, E, H = 8, 512, 512, 2
HD = E // H
S2 = 2 * T - 1


def rel_shift(m):
    b, h, t, p = m.shape
    mp = np.pad(m, ((0, 0), (0, 0), (0, 0), (1, 0)))
    mp = mp.reshape(b, h, p + 1, t)[:, :, 1:, :]
    return mp.reshape(b, h, t, p)[..., : p // 2 + 1]


def setup_inputs():
    s = mx_kscale(E)
    return {"q_u": bf(np.random.standard_normal((B, T, H, HD)) * 1.4),
            "k": bf(np.random.standard_normal((B, T, H, HD))),
            "matrix_bd": bf(np.random.standard_normal((B, H, T, S2)) * 1.4 * np.sqrt(HD)),
            "x": bf(np.random.standard_normal((B, T, E)) * s),
            "Wv": bf(np.random.standard_normal((E, E)) / np.sqrt(E) / s[None, :]),
            "bv": bf(np.random.standard_normal(E) * 0.3)}


def reference(q_u, k, matrix_bd, x, Wv, bv):
    v = (mxq(f64(x), 2, "e4m3") @ mxq(f64(Wv), 1, "e4m3").T) + f64(bv)
    v = v.reshape(B, T, H, HD).transpose(0, 2, 1, 3)
    matrix_ac = f64(q_u).transpose(0, 2, 1, 3) @ f64(k).transpose(0, 2, 3, 1)
    score = (matrix_ac + rel_shift(f64(matrix_bd))) * (1.0 / np.sqrt(HD))
    e = np.exp(score - score.max(-1, keepdims=True))
    o = (mxq(e, 3, "e4m3") @ mxq(v, 2, "e4m3")) / e.sum(-1, keepdims=True)
    return o.transpose(0, 2, 1, 3).reshape(B, T, E)

@@ -1,0 +1,218 @@
+from contextlib import ExitStack
+
+import concourse.mybir as mybir
+from concourse.masks import make_identity
+
+F32 = mybir.dt.float32
+BF16 = mybir.dt.bfloat16
+U32 = mybir.dt.uint32
+U8 = mybir.dt.uint8
+FP8X4 = mybir.dt.float8_e4m3fn_x4
+ALU = mybir.AluOpType
+ACT = mybir.ActivationFunctionType
+AXIS = mybir.AxisListType
+
+B, T, E, H = 8, 512, 512, 2
+HD = E // H
+P = 128
+NB = T // P
+REL = 2 * T - 1
+SCALE = 1.0 / 16.0
+GROUPS = B * H
+
+FLOPS = 3 * 2 * B * T * T * E
+BYTES = 2 * (3 * B * T * E + B * H * T * T + E * E + E) + 4 * B * T * E
+
+
+def tile_attentionforonnx_pa_t_kernel(tc, q_u, k, matrix_bd, x, Wv, bv, out):
+    nc = tc.nc
+    with ExitStack() as stack:
+        const = stack.enter_context(tc.tile_pool(name="const", bufs=1))
+        io = stack.enter_context(tc.tile_pool(name="io", bufs=3))
+        work = stack.enter_context(tc.tile_pool(name="work", bufs=2))
+        psum_score = stack.enter_context(tc.psum_pool(name="psum_score", bufs=4))
+        psum_turn = stack.enter_context(tc.psum_pool(name="psum_turn", bufs=2))
+        psum_mx = stack.enter_context(tc.psum_pool(name="psum_mx", bufs=2))
+        stack.enter_context(tc.manual_schedule())
+
+        x_rows, k_rows, q_rows, bd_rows = {}, {}, {}, {}
+        x_mx, v_mx, e_mx = {}, {}, {}
+        vT_rows, qT, kT = {}, {}, {}
+        score, shift, recip, o_rows = {}, {}, {}, {}
+
+        ident_f32 = const.tile([P, P], F32)
+        make_identity(nc, ident_f32[:])
+        ident_bf16 = const.tile([P, P], BF16)
+        nc.vector.tensor_copy(out=ident_bf16[:], in_=ident_f32[:])
+
+        def pack_for_mx(rows, name, bufs):
+            words = rows.bitcast(F32)
+            grouped = work.tile([P, NB * P * 4], BF16, tag="grouped", bufs=3, align_bytes=64)
+            grouped_words = grouped[:].bitcast(F32).rearrange("p (i r u) -> p i r u", i=NB, u=2)
+            for half in range(NB // 2):
+                turned = psum_turn.tile([P, 2, 2, P], F32, tag="turned")
+                for i in range(2):
+                    for u in range(2):
+                        nc.tensor.transpose(
+                            out=turned[:, i, u, :],
+                            in_=words[:, 2 * half + i, u * P : (u + 1) * P],
+                            identity=ident_f32[:],
+                        )
+                nc.scalar.copy(
+                    out=grouped_words[:, 2 * half : 2 * half + 2],
+                    in_=turned[:].rearrange("p i u r -> p i r u"),
+                )
+            codes = work.tile([P, NB * P], U32, tag=name + "_codes", bufs=bufs, align_bytes=64)
+            scales = work.tile([P, NB * P], U8, tag=name + "_scales", bufs=bufs, align_bytes=64)
+            nc.vector.quantize_mx(out=codes[:].bitcast(FP8X4), scales=scales[:], in_=grouped[:])
+            return codes, scales
+
+        def heads_to_partitions(rows, name):
+            words = rows.bitcast(F32)
+            turned_words = work.tile([P, H, NB, P], F32, tag=name)
+            for h in range(H):
+                turned = psum_turn.tile([P, NB, P], F32, tag="turned")
+                for i in range(NB):
+                    nc.tensor.transpose(
+                        out=turned[:, i, :],
+                        in_=words[:, i, h * P : (h + 1) * P],
+                        identity=ident_f32[:],
+                    )
+                nc.scalar.copy(out=turned_words[:, h], in_=turned[:])
+            return turned_words[:].bitcast(BF16).rearrange("p h i (r e) -> p h (i r) e", e=2)
+
+        def load(b):
+            x_rows[b] = io.tile([P, NB, E], BF16, name="x_rows")
+            nc.sync.dma_start(out=x_rows[b][:], in_=x[b].rearrange("(i p) c -> p i c", p=P))
+            k_rows[b] = io.tile([P, NB, E], BF16, name="k_rows")
+            nc.sync.dma_start(out=k_rows[b][:], in_=k[b].rearrange("(i p) h d -> p i (h d)", p=P))
+            q_rows[b] = io.tile([P, NB, E], BF16, name="q_rows")
+            nc.sync.dma_start(
+                out=q_rows[b][:], in_=q_u[b].rearrange("(p j) h d -> p j (h d)", j=NB)
+            )
+            bd_rows[b] = io.tile([P, H, NB, T], BF16, name="bd_rows")
+            for h in range(H):
+                flat = matrix_bd[b, h].rearrange("t r -> (t r)")
+                skewed = flat[T - 1 : T - 1 + T * (REL - 1)].rearrange(
+                    "(p j c) -> p j c", j=NB, c=REL - 1
+                )
+                nc.sync.dma_start(out=bd_rows[b][:, h], in_=skewed[:, :, 0:T])
+
+        def project_v(b):
+            x_codes, x_scales = x_mx[b]
+            vT_rows[b] = work.tile([P, NB, T], BF16, name="vT_rows")
+            for f in range(NB):
+                vT_acc = psum_mx.tile([P, T], F32, tag="mx")
+                nc.tensor.matmul_mx(
+                    out=vT_acc[:],
+                    lhsT=w_codes[:, f * P : (f + 1) * P].bitcast(FP8X4),
+                    lhsT_scale=w_scales[:, f * P : (f + 1) * P],
+                    rhs=x_codes[:].bitcast(FP8X4),
+                    rhs_scale=x_scales[:],
+                    start=True,
+                    stop=True,
+                )
+                nc.scalar.activation(
+                    out=vT_rows[b][:, f, :],
+                    in_=vT_acc[:],
+                    func=ACT.Identity,
+                    bias=bias_col[:, f : f + 1],
+                )
+
+        def scores(g):
+            b, h = divmod(g, H)
+            score[g] = work.tile([P, NB, T], F32, name="score")
+            for j in range(NB):
+                ac = psum_score.tile([P, T], F32)
+                for e in range(2):
+                    nc.tensor.matmul(
+                        out=ac[:],
+                        lhsT=qT[b][:, h, j * P : (j + 1) * P, e],
+                        rhs=kT[b][:, h, :, e],
+                        start=(e == 0),
+                        stop=(e == 1),
+                    )
+                nc.vector.tensor_tensor(
+                    out=score[g][:, j, :], in0=ac[:], in1=bd_rows[b][:, h, j, :], op=ALU.add
+                )
+            top = work.tile([P, NB], F32)
+            nc.vector.tensor_reduce(out=top[:], in_=score[g][:], axis=AXIS.X, op=ALU.max)
+            shift[g] = work.tile([P, NB], F32, name="shift")
+            nc.vector.tensor_scalar_mul(out=shift[g][:], in0=top[:], scalar1=-SCALE)
+
+        def softmax_numerator(g):
+            e_rows = work.tile([P, NB, T], BF16)
+            rowsum = work.tile([P, NB], F32)
+            for j in range(NB):
+                nc.scalar.activation(
+                    out=e_rows[:, j, :],
+                    in_=score[g][:, j, :],
+                    func=ACT.Exp,
+                    bias=shift[g][:, j : j + 1],
+                    scale=SCALE,
+                    accum_out=rowsum[:, j : j + 1],
+                )
+            recip[g] = work.tile([P, NB], F32, name="recip")
+            nc.vector.reciprocal(out=recip[g][:], in_=rowsum[:])
+            e_mx[g] = pack_for_mx(e_rows[:], "e", 2)
+
+        def output(g):
+            b, h = divmod(g, H)
+            e_codes, e_scales = e_mx[g]
+            v_codes, v_scales = v_mx[b]
+            if h == 0:
+                o_rows[b] = work.tile([P, NB, E], F32, name="o_rows")
+            for half in range(NB // 2):
+                o_acc = psum_mx.tile([P, 2, HD], F32, tag="mx")
+                for i in range(2):
+                    j = 2 * half + i
+                    nc.tensor.matmul_mx(
+                        out=o_acc[:, i, :],
+                        lhsT=e_codes[:, j * P : (j + 1) * P].bitcast(FP8X4),
+                        lhsT_scale=e_scales[:, j * P : (j + 1) * P],
+                        rhs=v_codes[:, h * HD : (h + 1) * HD].bitcast(FP8X4),
+                        rhs_scale=v_scales[:, h * HD : (h + 1) * HD],
+                        start=True,
+                        stop=True,
+                    )
+                nc.vector.tensor_tensor(
+                    out=o_rows[b][:, 2 * half : 2 * half + 2, h * HD : (h + 1) * HD],
+                    in0=o_acc[:],
+                    in1=recip[g][:, 2 * half : 2 * half + 2].unsqueeze(2).to_broadcast([P, 2, HD]),
+                    op=ALU.mult,
+                )
+            if h == H - 1:
+                nc.sync.dma_start(out=out[b].rearrange("(p j) c -> p j c", j=NB), in_=o_rows[b][:])
+
+        bv_rows = const.tile([P, P], BF16)
+        nc.vector.memset(bv_rows[:], 0.0)
+        nc.sync.dma_start(out=bv_rows[0:NB, :], in_=bv.rearrange("(f c) -> f c", c=P))
+        w_rows = const.tile([P, NB, E], BF16)
+        nc.sync.dma_start(out=w_rows[:], in_=Wv.rearrange("(f p) c -> p f c", p=P))
+        load(0)
+        bv_turned = psum_turn.tile([P, P], BF16, tag="turned")
+        nc.tensor.transpose(out=bv_turned[:], in_=bv_rows[:], identity=ident_bf16[:])
+        bias_col = const.tile([P, NB], F32)
+        nc.vector.tensor_copy(out=bias_col[:], in_=bv_turned[:, 0:NB])
+        w_codes, w_scales = pack_for_mx(w_rows[:], "w", 1)
+
+        for step in range(-2, GROUPS + 1):
+            b, odd = divmod(step, 2)
+            if 0 <= step < GROUPS:
+                scores(step)
+            if 0 <= step - 1 < GROUPS:
+                softmax_numerator(step - 1)
+            if odd:
+                if b + 1 < B:
+                    qT[b + 1] = heads_to_partitions(q_rows[b + 1][:], "qT")
+                    project_v(b + 1)
+            else:
+                if b + 2 < B:
+                    load(b + 2)
+                if 0 <= b < B:
+                    v_mx[b] = pack_for_mx(vT_rows[b][:], "v", 2)
+                if b + 1 < B:
+                    x_mx[b + 1] = pack_for_mx(x_rows[b + 1][:], "x", 2)
+                    kT[b + 1] = heads_to_partitions(k_rows[b + 1][:], "kT")
+            if 0 <= step - 1 < GROUPS:
+                output(step - 1)

@@ -19,6 +19,7 @@ NB = T // P
 REL = 2 * T - 1
 SCALE = 1.0 / 16.0
 GROUPS = B * H
+OUTPUT_LAG = 2
 
 FLOPS = 3 * 2 * B * T * T * E
 BYTES = 2 * (3 * B * T * E + B * H * T * T + E * E + E) + 4 * B * T * E
@@ -31,14 +32,13 @@ def tile_attentionforonnx_pa_t_kernel(tc, q_u, k, matrix_bd, x, Wv, bv, out):
         io = stack.enter_context(tc.tile_pool(name="io", bufs=3))
         work = stack.enter_context(tc.tile_pool(name="work", bufs=2))
         psum_score = stack.enter_context(tc.psum_pool(name="psum_score", bufs=4))
-        psum_turn = stack.enter_context(tc.psum_pool(name="psum_turn", bufs=2))
-        psum_mx = stack.enter_context(tc.psum_pool(name="psum_mx", bufs=2))
+        psum_ring = stack.enter_context(tc.psum_pool(name="psum_ring", bufs=4))
         stack.enter_context(tc.manual_schedule())
 
         x_rows, k_rows, q_rows, bd_rows = {}, {}, {}, {}
         x_mx, v_mx, e_mx = {}, {}, {}
         vT_rows, qT, kT = {}, {}, {}
-        score, shift, recip, o_rows = {}, {}, {}, {}
+        score, shift, e_rows, recip = {}, {}, {}, {}
 
         ident_f32 = const.tile([P, P], F32)
         make_identity(nc, ident_f32[:])
@@ -50,7 +50,7 @@ def tile_attentionforonnx_pa_t_kernel(tc, q_u, k, matrix_bd, x, Wv, bv, out):
             grouped = work.tile([P, NB * P * 4], BF16, tag="grouped", bufs=3, align_bytes=64)
             grouped_words = grouped[:].bitcast(F32).rearrange("p (i r u) -> p i r u", i=NB, u=2)
             for half in range(NB // 2):
-                turned = psum_turn.tile([P, 2, 2, P], F32, tag="turned")
+                turned = psum_ring.tile([P, 2, 2, P], F32, tag="ring")
                 for i in range(2):
                     for u in range(2):
                         nc.tensor.transpose(
@@ -71,7 +71,7 @@ def tile_attentionforonnx_pa_t_kernel(tc, q_u, k, matrix_bd, x, Wv, bv, out):
             words = rows.bitcast(F32)
             turned_words = work.tile([P, H, NB, P], F32, tag=name)
             for h in range(H):
-                turned = psum_turn.tile([P, NB, P], F32, tag="turned")
+                turned = psum_ring.tile([P, NB, P], F32, tag="ring")
                 for i in range(NB):
                     nc.tensor.transpose(
                         out=turned[:, i, :],
@@ -81,28 +81,34 @@ def tile_attentionforonnx_pa_t_kernel(tc, q_u, k, matrix_bd, x, Wv, bv, out):
                 nc.scalar.copy(out=turned_words[:, h], in_=turned[:])
             return turned_words[:].bitcast(BF16).rearrange("p h i (r e) -> p h (i r) e", e=2)
 
-        def load(b):
-            x_rows[b] = io.tile([P, NB, E], BF16, name="x_rows")
-            nc.sync.dma_start(out=x_rows[b][:], in_=x[b].rearrange("(i p) c -> p i c", p=P))
+        def load_k(b):
             k_rows[b] = io.tile([P, NB, E], BF16, name="k_rows")
             nc.sync.dma_start(out=k_rows[b][:], in_=k[b].rearrange("(i p) h d -> p i (h d)", p=P))
+
+        def load_q(b):
             q_rows[b] = io.tile([P, NB, E], BF16, name="q_rows")
             nc.sync.dma_start(
                 out=q_rows[b][:], in_=q_u[b].rearrange("(p j) h d -> p j (h d)", j=NB)
             )
-            bd_rows[b] = io.tile([P, H, NB, T], BF16, name="bd_rows")
-            for h in range(H):
-                flat = matrix_bd[b, h].rearrange("t r -> (t r)")
-                skewed = flat[T - 1 : T - 1 + T * (REL - 1)].rearrange(
-                    "(p j c) -> p j c", j=NB, c=REL - 1
-                )
-                nc.sync.dma_start(out=bd_rows[b][:, h], in_=skewed[:, :, 0:T])
+
+        def load_x(b):
+            x_rows[b] = io.tile([P, NB, E], BF16, name="x_rows")
+            nc.sync.dma_start(out=x_rows[b][:], in_=x[b].rearrange("(i p) c -> p i c", p=P))
+
+        def load_bd(g):
+            b, h = divmod(g, H)
+            flat = matrix_bd[b, h].rearrange("t r -> (t r)")
+            skewed = flat[T - 1 : T - 1 + T * (REL - 1)].rearrange(
+                "(p j c) -> p j c", j=NB, c=REL - 1
+            )
+            bd_rows[g] = io.tile([P, NB, T], BF16, name="bd_rows", bufs=3 * H)
+            nc.sync.dma_start(out=bd_rows[g][:], in_=skewed[:, :, 0:T])
 
         def project_v(b):
             x_codes, x_scales = x_mx[b]
             vT_rows[b] = work.tile([P, NB, T], BF16, name="vT_rows")
             for f in range(NB):
-                vT_acc = psum_mx.tile([P, T], F32, tag="mx")
+                vT_acc = psum_ring.tile([P, T], F32, tag="ring")
                 nc.tensor.matmul_mx(
                     out=vT_acc[:],
                     lhsT=w_codes[:, f * P : (f + 1) * P].bitcast(FP8X4),
@@ -133,37 +139,35 @@ def tile_attentionforonnx_pa_t_kernel(tc, q_u, k, matrix_bd, x, Wv, bv, out):
                         stop=(e == 1),
                     )
                 nc.vector.tensor_tensor(
-                    out=score[g][:, j, :], in0=ac[:], in1=bd_rows[b][:, h, j, :], op=ALU.add
+                    out=score[g][:, j, :], in0=ac[:], in1=bd_rows[g][:, j, :], op=ALU.add
                 )
             top = work.tile([P, NB], F32)
             nc.vector.tensor_reduce(out=top[:], in_=score[g][:], axis=AXIS.X, op=ALU.max)
             shift[g] = work.tile([P, NB], F32, name="shift")
             nc.vector.tensor_scalar_mul(out=shift[g][:], in0=top[:], scalar1=-SCALE)
 
-        def softmax_numerator(g):
-            e_rows = work.tile([P, NB, T], BF16)
+        def exponentials(g):
+            e_rows[g] = work.tile([P, NB, T], BF16, name="e_rows")
             rowsum = work.tile([P, NB], F32)
             for j in range(NB):
                 nc.scalar.activation(
-                    out=e_rows[:, j, :],
+                    out=e_rows[g][:, j, :],
                     in_=score[g][:, j, :],
                     func=ACT.Exp,
                     bias=shift[g][:, j : j + 1],
                     scale=SCALE,
                     accum_out=rowsum[:, j : j + 1],
                 )
-            recip[g] = work.tile([P, NB], F32, name="recip")
+            recip[g] = work.tile([P, NB], F32, name="recip", bufs=OUTPUT_LAG + 1)
             nc.vector.reciprocal(out=recip[g][:], in_=rowsum[:])
-            e_mx[g] = pack_for_mx(e_rows[:], "e", 2)
 
         def output(g):
             b, h = divmod(g, H)
             e_codes, e_scales = e_mx[g]
             v_codes, v_scales = v_mx[b]
-            if h == 0:
-                o_rows[b] = work.tile([P, NB, E], F32, name="o_rows")
+            o_rows = work.tile([P, NB, HD], F32, bufs=3)
             for half in range(NB // 2):
-                o_acc = psum_mx.tile([P, 2, HD], F32, tag="mx")
+                o_acc = psum_ring.tile([P, 2, HD], F32, tag="ring")
                 for i in range(2):
                     j = 2 * half + i
                     nc.tensor.matmul_mx(
@@ -176,43 +180,64 @@ def tile_attentionforonnx_pa_t_kernel(tc, q_u, k, matrix_bd, x, Wv, bv, out):
                         stop=True,
                     )
                 nc.vector.tensor_tensor(
-                    out=o_rows[b][:, 2 * half : 2 * half + 2, h * HD : (h + 1) * HD],
+                    out=o_rows[:, 2 * half : 2 * half + 2, :],
                     in0=o_acc[:],
                     in1=recip[g][:, 2 * half : 2 * half + 2].unsqueeze(2).to_broadcast([P, 2, HD]),
                     op=ALU.mult,
                 )
-            if h == H - 1:
-                nc.sync.dma_start(out=out[b].rearrange("(p j) c -> p j c", j=NB), in_=o_rows[b][:])
+            nc.sync.dma_start(
+                out=out[b, :, h * HD : (h + 1) * HD].rearrange("(p j) c -> p j c", j=NB),
+                in_=o_rows[:],
+            )
 
+        load_k(0)
+        load_q(0)
+        load_bd(0)
+        w_rows = const.tile([P, NB, E], BF16)
+        nc.sync.dma_start(out=w_rows[:], in_=Wv.rearrange("(f p) c -> p f c", p=P))
+        load_x(0)
         bv_rows = const.tile([P, P], BF16)
         nc.vector.memset(bv_rows[:], 0.0)
         nc.sync.dma_start(out=bv_rows[0:NB, :], in_=bv.rearrange("(f c) -> f c", c=P))
-        w_rows = const.tile([P, NB, E], BF16)
-        nc.sync.dma_start(out=w_rows[:], in_=Wv.rearrange("(f p) c -> p f c", p=P))
-        load(0)
-        bv_turned = psum_turn.tile([P, P], BF16, tag="turned")
-        nc.tensor.transpose(out=bv_turned[:], in_=bv_rows[:], identity=ident_bf16[:])
-        bias_col = const.tile([P, NB], F32)
-        nc.vector.tensor_copy(out=bias_col[:], in_=bv_turned[:, 0:NB])
-        w_codes, w_scales = pack_for_mx(w_rows[:], "w", 1)
+        load_bd(1)
+        load_k(1)
+        load_q(1)
+        load_bd(2)
+        load_bd(3)
+        load_x(1)
 
-        for step in range(-2, GROUPS + 1):
+        kT[0] = heads_to_partitions(k_rows[0][:], "kT")
+        qT[0] = heads_to_partitions(q_rows[0][:], "qT")
+
+        for step in range(GROUPS + OUTPUT_LAG):
             b, odd = divmod(step, 2)
-            if 0 <= step < GROUPS:
+            if not odd and b + 2 < B:
+                load_k(b + 2)
+                load_q(b + 2)
+                load_bd(H * (b + 2))
+                load_bd(H * (b + 2) + 1)
+                load_x(b + 2)
+            if step < GROUPS:
                 scores(step)
             if 0 <= step - 1 < GROUPS:
-                softmax_numerator(step - 1)
-            if odd:
-                if b + 1 < B:
-                    qT[b + 1] = heads_to_partitions(q_rows[b + 1][:], "qT")
-                    project_v(b + 1)
-            else:
-                if b + 2 < B:
-                    load(b + 2)
-                if 0 <= b < B:
-                    v_mx[b] = pack_for_mx(vT_rows[b][:], "v", 2)
-                if b + 1 < B:
-                    x_mx[b + 1] = pack_for_mx(x_rows[b + 1][:], "x", 2)
-                    kT[b + 1] = heads_to_partitions(k_rows[b + 1][:], "kT")
+                exponentials(step - 1)
+            if not odd and 0 <= b - 1 < B:
+                v_mx[b - 1] = pack_for_mx(vT_rows[b - 1][:], "v", 2)
+            if odd and b + 1 < B:
+                qT[b + 1] = heads_to_partitions(q_rows[b + 1][:], "qT")
             if 0 <= step - 1 < GROUPS:
-                output(step - 1)
+                e_mx[step - 1] = pack_for_mx(e_rows[step - 1][:], "e", OUTPUT_LAG)
+            if step == 0:
+                w_codes, w_scales = pack_for_mx(w_rows[:], "w", 1)
+                bv_turned = psum_ring.tile([P, P], BF16, tag="ring")
+                nc.tensor.transpose(out=bv_turned[:], in_=bv_rows[:], identity=ident_bf16[:])
+                bias_col = const.tile([P, NB], F32)
+                nc.vector.tensor_copy(out=bias_col[:], in_=bv_turned[:, 0:NB])
+            if not odd and b < B:
+                x_mx[b] = pack_for_mx(x_rows[b][:], "x", 2)
+            if not odd and b + 1 < B:
+                kT[b + 1] = heads_to_partitions(k_rows[b + 1][:], "kT")
+            if odd and b < B:
+                project_v(b)
+            if 0 <= step - OUTPUT_LAG < GROUPS:
+                output(step - OUTPUT_LAG)

@@ -38,7 +38,7 @@ def tile_attentionforonnx_pa_t_kernel(tc, q_u, k, matrix_bd, x, Wv, bv, out):
         x_rows, k_rows, q_rows, bd_rows = {}, {}, {}, {}
         x_mx, v_mx, e_mx = {}, {}, {}
         vT_rows, qT, kT = {}, {}, {}
-        score, shift, e_rows, recip = {}, {}, {}, {}
+        ac, score, shift, e_rows, recip = {}, {}, {}, {}, {}
 
         ident_f32 = const.tile([P, P], F32)
         make_identity(nc, ident_f32[:])
@@ -104,10 +104,9 @@ def tile_attentionforonnx_pa_t_kernel(tc, q_u, k, matrix_bd, x, Wv, bv, out):
             bd_rows[g] = io.tile([P, NB, T], BF16, name="bd_rows", bufs=3 * H)
             nc.sync.dma_start(out=bd_rows[g][:], in_=skewed[:, :, 0:T])
 
-        def project_v(b):
+        def project_v(b, blocks):
             x_codes, x_scales = x_mx[b]
-            vT_rows[b] = work.tile([P, NB, T], BF16, name="vT_rows")
-            for f in range(NB):
+            for f in blocks:
                 vT_acc = psum_ring.tile([P, T], F32, tag="ring")
                 nc.tensor.matmul_mx(
                     out=vT_acc[:],
@@ -125,21 +124,23 @@ def tile_attentionforonnx_pa_t_kernel(tc, q_u, k, matrix_bd, x, Wv, bv, out):
                     bias=bias_col[:, f : f + 1],
                 )
 
-        def scores(g):
+        def score_matmuls(g, j):
             b, h = divmod(g, H)
+            ac[g, j] = psum_score.tile([P, T], F32, name="ac")
+            for e in range(2):
+                nc.tensor.matmul(
+                    out=ac[g, j][:],
+                    lhsT=qT[b][:, h, j * P : (j + 1) * P, e],
+                    rhs=kT[b][:, h, :, e],
+                    start=(e == 0),
+                    stop=(e == 1),
+                )
+
+        def score_sums(g):
             score[g] = work.tile([P, NB, T], F32, name="score")
             for j in range(NB):
-                ac = psum_score.tile([P, T], F32)
-                for e in range(2):
-                    nc.tensor.matmul(
-                        out=ac[:],
-                        lhsT=qT[b][:, h, j * P : (j + 1) * P, e],
-                        rhs=kT[b][:, h, :, e],
-                        start=(e == 0),
-                        stop=(e == 1),
-                    )
                 nc.vector.tensor_tensor(
-                    out=score[g][:, j, :], in0=ac[:], in1=bd_rows[g][:, j, :], op=ALU.add
+                    out=score[g][:, j, :], in0=ac[g, j][:], in1=bd_rows[g][:, j, :], op=ALU.add
                 )
             top = work.tile([P, NB], F32)
             nc.vector.tensor_reduce(out=top[:], in_=score[g][:], axis=AXIS.X, op=ALU.max)
@@ -202,42 +203,56 @@ def tile_attentionforonnx_pa_t_kernel(tc, q_u, k, matrix_bd, x, Wv, bv, out):
         load_bd(1)
         load_k(1)
         load_q(1)
+        load_x(1)
         load_bd(2)
         load_bd(3)
-        load_x(1)
 
         kT[0] = heads_to_partitions(k_rows[0][:], "kT")
         qT[0] = heads_to_partitions(q_rows[0][:], "qT")
+        for j in range(NB):
+            score_matmuls(0, j)
 
         for step in range(GROUPS + OUTPUT_LAG):
             b, odd = divmod(step, 2)
             if not odd and b + 2 < B:
                 load_k(b + 2)
                 load_q(b + 2)
+                load_x(b + 2)
                 load_bd(H * (b + 2))
                 load_bd(H * (b + 2) + 1)
-                load_x(b + 2)
             if step < GROUPS:
-                scores(step)
+                score_sums(step)
             if 0 <= step - 1 < GROUPS:
                 exponentials(step - 1)
             if not odd and 0 <= b - 1 < B:
                 v_mx[b - 1] = pack_for_mx(vT_rows[b - 1][:], "v", 2)
             if odd and b + 1 < B:
-                qT[b + 1] = heads_to_partitions(q_rows[b + 1][:], "qT")
+                x_mx[b + 1] = pack_for_mx(x_rows[b + 1][:], "x", 2)
+            if step + 1 < GROUPS:
+                score_matmuls(step + 1, 0)
             if 0 <= step - 1 < GROUPS:
                 e_mx[step - 1] = pack_for_mx(e_rows[step - 1][:], "e", OUTPUT_LAG)
+            if step + 1 < GROUPS:
+                score_matmuls(step + 1, 1)
             if step == 0:
                 w_codes, w_scales = pack_for_mx(w_rows[:], "w", 1)
                 bv_turned = psum_ring.tile([P, P], BF16, tag="ring")
                 nc.tensor.transpose(out=bv_turned[:], in_=bv_rows[:], identity=ident_bf16[:])
                 bias_col = const.tile([P, NB], F32)
                 nc.vector.tensor_copy(out=bias_col[:], in_=bv_turned[:, 0:NB])
-            if not odd and b < B:
-                x_mx[b] = pack_for_mx(x_rows[b][:], "x", 2)
+                x_mx[0] = pack_for_mx(x_rows[0][:], "x", 2)
             if not odd and b + 1 < B:
                 kT[b + 1] = heads_to_partitions(k_rows[b + 1][:], "kT")
             if odd and b < B:
-                project_v(b)
+                vT_rows[b] = work.tile([P, NB, T], BF16, name="vT_rows")
+                project_v(b, range(0, NB // 2))
+            if step + 1 < GROUPS:
+                score_matmuls(step + 1, 2)
+            if not odd and b + 1 < B:
+                qT[b + 1] = heads_to_partitions(q_rows[b + 1][:], "qT")
+            if odd and b < B:
+                project_v(b, range(NB // 2, NB))
             if 0 <= step - OUTPUT_LAG < GROUPS:
                 output(step - OUTPUT_LAG)
+            if step + 1 < GROUPS:
+                score_matmuls(step + 1, 3)

@@ -33,12 +33,11 @@ def tile_attentionforonnx_pa_t_kernel(tc, q_u, k, matrix_bd, x, Wv, bv, out):
         work = stack.enter_context(tc.tile_pool(name="work", bufs=2))
         psum_score = stack.enter_context(tc.psum_pool(name="psum_score", bufs=4))
         psum_ring = stack.enter_context(tc.psum_pool(name="psum_ring", bufs=4))
-        stack.enter_context(tc.manual_schedule())
 
         x_rows, k_rows, q_rows, bd_rows = {}, {}, {}, {}
         x_mx, v_mx, e_mx = {}, {}, {}
         vT_rows, qT, kT = {}, {}, {}
-        ac, score, shift, e_rows, recip = {}, {}, {}, {}, {}
+        score, shift, e_rows, recip = {}, {}, {}, {}
 
         ident_f32 = const.tile([P, P], F32)
         make_identity(nc, ident_f32[:])
@@ -104,9 +103,10 @@ def tile_attentionforonnx_pa_t_kernel(tc, q_u, k, matrix_bd, x, Wv, bv, out):
             bd_rows[g] = io.tile([P, NB, T], BF16, name="bd_rows", bufs=3 * H)
             nc.sync.dma_start(out=bd_rows[g][:], in_=skewed[:, :, 0:T])
 
-        def project_v(b, blocks):
+        def project_v(b):
             x_codes, x_scales = x_mx[b]
-            for f in blocks:
+            vT_rows[b] = work.tile([P, NB, T], BF16, name="vT_rows")
+            for f in range(NB):
                 vT_acc = psum_ring.tile([P, T], F32, tag="ring")
                 nc.tensor.matmul_mx(
                     out=vT_acc[:],
@@ -124,23 +124,21 @@ def tile_attentionforonnx_pa_t_kernel(tc, q_u, k, matrix_bd, x, Wv, bv, out):
                     bias=bias_col[:, f : f + 1],
                 )
 
-        def score_matmuls(g, j):
+        def scores(g):
             b, h = divmod(g, H)
-            ac[g, j] = psum_score.tile([P, T], F32, name="ac")
-            for e in range(2):
-                nc.tensor.matmul(
-                    out=ac[g, j][:],
-                    lhsT=qT[b][:, h, j * P : (j + 1) * P, e],
-                    rhs=kT[b][:, h, :, e],
-                    start=(e == 0),
-                    stop=(e == 1),
-                )
-
-        def score_sums(g):
             score[g] = work.tile([P, NB, T], F32, name="score")
             for j in range(NB):
+                ac = psum_score.tile([P, T], F32)
+                for e in range(2):
+                    nc.tensor.matmul(
+                        out=ac[:],
+                        lhsT=qT[b][:, h, j * P : (j + 1) * P, e],
+                        rhs=kT[b][:, h, :, e],
+                        start=(e == 0),
+                        stop=(e == 1),
+                    )
                 nc.vector.tensor_tensor(
-                    out=score[g][:, j, :], in0=ac[g, j][:], in1=bd_rows[g][:, j, :], op=ALU.add
+                    out=score[g][:, j, :], in0=ac[:], in1=bd_rows[g][:, j, :], op=ALU.add
                 )
             top = work.tile([P, NB], F32)
             nc.vector.tensor_reduce(out=top[:], in_=score[g][:], axis=AXIS.X, op=ALU.max)
@@ -203,56 +201,42 @@ def tile_attentionforonnx_pa_t_kernel(tc, q_u, k, matrix_bd, x, Wv, bv, out):
         load_bd(1)
         load_k(1)
         load_q(1)
-        load_x(1)
         load_bd(2)
         load_bd(3)
+        load_x(1)
 
         kT[0] = heads_to_partitions(k_rows[0][:], "kT")
         qT[0] = heads_to_partitions(q_rows[0][:], "qT")
-        for j in range(NB):
-            score_matmuls(0, j)
 
         for step in range(GROUPS + OUTPUT_LAG):
             b, odd = divmod(step, 2)
             if not odd and b + 2 < B:
                 load_k(b + 2)
                 load_q(b + 2)
-                load_x(b + 2)
                 load_bd(H * (b + 2))
                 load_bd(H * (b + 2) + 1)
+                load_x(b + 2)
             if step < GROUPS:
-                score_sums(step)
+                scores(step)
             if 0 <= step - 1 < GROUPS:
                 exponentials(step - 1)
             if not odd and 0 <= b - 1 < B:
                 v_mx[b - 1] = pack_for_mx(vT_rows[b - 1][:], "v", 2)
             if odd and b + 1 < B:
-                x_mx[b + 1] = pack_for_mx(x_rows[b + 1][:], "x", 2)
-            if step + 1 < GROUPS:
-                score_matmuls(step + 1, 0)
+                qT[b + 1] = heads_to_partitions(q_rows[b + 1][:], "qT")
             if 0 <= step - 1 < GROUPS:
                 e_mx[step - 1] = pack_for_mx(e_rows[step - 1][:], "e", OUTPUT_LAG)
-            if step + 1 < GROUPS:
-                score_matmuls(step + 1, 1)
             if step == 0:
                 w_codes, w_scales = pack_for_mx(w_rows[:], "w", 1)
                 bv_turned = psum_ring.tile([P, P], BF16, tag="ring")
                 nc.tensor.transpose(out=bv_turned[:], in_=bv_rows[:], identity=ident_bf16[:])
                 bias_col = const.tile([P, NB], F32)
                 nc.vector.tensor_copy(out=bias_col[:], in_=bv_turned[:, 0:NB])
-                x_mx[0] = pack_for_mx(x_rows[0][:], "x", 2)
+            if not odd and b < B:
+                x_mx[b] = pack_for_mx(x_rows[b][:], "x", 2)
             if not odd and b + 1 < B:
                 kT[b + 1] = heads_to_partitions(k_rows[b + 1][:], "kT")
             if odd and b < B:
-                vT_rows[b] = work.tile([P, NB, T], BF16, name="vT_rows")
-                project_v(b, range(0, NB // 2))
-            if step + 1 < GROUPS:
-                score_matmuls(step + 1, 2)
-            if not odd and b + 1 < B:
-                qT[b + 1] = heads_to_partitions(q_rows[b + 1][:], "qT")
-            if odd and b < B:
-                project_v(b, range(NB // 2, NB))
+                project_v(b)
             if 0 <= step - OUTPUT_LAG < GROUPS:
                 output(step - OUTPUT_LAG)
-            if step + 1 < GROUPS:
-                score_matmuls(step + 1, 3)

@@ -19,6 +19,10 @@ NB = T // P
 REL = 2 * T - 1
 SCALE = 1.0 / 16.0
 GROUPS = B * H
+def blocks_added_by_tensor(g):
+    return 2 if g % 3 == 1 else 1
+
+
 OUTPUT_LAG = 2
 
 FLOPS = 3 * 2 * B * T * T * E
@@ -31,18 +35,25 @@ def tile_attentionforonnx_pa_t_kernel(tc, q_u, k, matrix_bd, x, Wv, bv, out):
         const = stack.enter_context(tc.tile_pool(name="const", bufs=1))
         io = stack.enter_context(tc.tile_pool(name="io", bufs=3))
         work = stack.enter_context(tc.tile_pool(name="work", bufs=2))
-        psum_score = stack.enter_context(tc.psum_pool(name="psum_score", bufs=4))
+        psum_score = stack.enter_context(tc.psum_pool(name="psum_score", bufs=2))
         psum_ring = stack.enter_context(tc.psum_pool(name="psum_ring", bufs=4))
 
         x_rows, k_rows, q_rows, bd_rows = {}, {}, {}, {}
         x_mx, v_mx, e_mx = {}, {}, {}
-        vT_rows, qT, kT = {}, {}, {}
+        v_grouped, qT, kT = {}, {}, {}
         score, shift, e_rows, recip = {}, {}, {}, {}
 
         ident_f32 = const.tile([P, P], F32)
         make_identity(nc, ident_f32[:])
+
         ident_bf16 = const.tile([P, P], BF16)
         nc.vector.tensor_copy(out=ident_bf16[:], in_=ident_f32[:])
+
+        def quantize(grouped, name, bufs):
+            codes = work.tile([P, NB * P], U32, tag=name + "_codes", bufs=bufs, align_bytes=64)
+            scales = work.tile([P, NB * P], U8, tag=name + "_scales", bufs=bufs, align_bytes=64)
+            nc.vector.quantize_mx(out=codes[:].bitcast(FP8X4), scales=scales[:], in_=grouped)
+            return codes, scales
 
         def pack_for_mx(rows, name, bufs):
             words = rows.bitcast(F32)
@@ -61,10 +72,7 @@ def tile_attentionforonnx_pa_t_kernel(tc, q_u, k, matrix_bd, x, Wv, bv, out):
                     out=grouped_words[:, 2 * half : 2 * half + 2],
                     in_=turned[:].rearrange("p i u r -> p i r u"),
                 )
-            codes = work.tile([P, NB * P], U32, tag=name + "_codes", bufs=bufs, align_bytes=64)
-            scales = work.tile([P, NB * P], U8, tag=name + "_scales", bufs=bufs, align_bytes=64)
-            nc.vector.quantize_mx(out=codes[:].bitcast(FP8X4), scales=scales[:], in_=grouped[:])
-            return codes, scales
+            return quantize(grouped[:], name, bufs)
 
         def heads_to_partitions(rows, name):
             words = rows.bitcast(F32)
@@ -92,7 +100,10 @@ def tile_attentionforonnx_pa_t_kernel(tc, q_u, k, matrix_bd, x, Wv, bv, out):
 
         def load_x(b):
             x_rows[b] = io.tile([P, NB, E], BF16, name="x_rows")
-            nc.sync.dma_start(out=x_rows[b][:], in_=x[b].rearrange("(i p) c -> p i c", p=P))
+            nc.sync.dma_start(
+                out=x_rows[b][:].rearrange("p (u e) c -> p u (e c)", u=2),
+                in_=x[b].rearrange("(u p e) c -> p u (e c)", u=2, e=2),
+            )
 
         def load_bd(g):
             b, h = divmod(g, H)
@@ -105,43 +116,62 @@ def tile_attentionforonnx_pa_t_kernel(tc, q_u, k, matrix_bd, x, Wv, bv, out):
 
         def project_v(b):
             x_codes, x_scales = x_mx[b]
-            vT_rows[b] = work.tile([P, NB, T], BF16, name="vT_rows")
+            v_grouped[b] = work.tile([P, E, NB], BF16, name="v_grouped", align_bytes=64)
             for f in range(NB):
-                vT_acc = psum_ring.tile([P, T], F32, tag="ring")
-                nc.tensor.matmul_mx(
-                    out=vT_acc[:],
-                    lhsT=w_codes[:, f * P : (f + 1) * P].bitcast(FP8X4),
-                    lhsT_scale=w_scales[:, f * P : (f + 1) * P],
-                    rhs=x_codes[:].bitcast(FP8X4),
-                    rhs_scale=x_scales[:],
-                    start=True,
-                    stop=True,
-                )
-                nc.scalar.activation(
-                    out=vT_rows[b][:, f, :],
-                    in_=vT_acc[:],
-                    func=ACT.Identity,
-                    bias=bias_col[:, f : f + 1],
+                features = slice(f * P, (f + 1) * P)
+                v_acc = psum_ring.tile([P, NB, P], F32, tag="ring")
+                for t in range(NB):
+                    nc.tensor.matmul_mx(
+                        out=v_acc[:, t, :],
+                        lhsT=x_codes[:, t * P : (t + 1) * P].bitcast(FP8X4),
+                        lhsT_scale=x_scales[:, t * P : (t + 1) * P],
+                        rhs=w_codes[:, features].bitcast(FP8X4),
+                        rhs_scale=w_scales[:, features],
+                        start=True,
+                        stop=True,
+                    )
+                nc.vector.tensor_tensor(
+                    out=v_grouped[b][:, features, :],
+                    in0=v_acc[:].rearrange("p t f -> p f t"),
+                    in1=bias_rows[:, features].unsqueeze(2).to_broadcast([P, P, NB]),
+                    op=ALU.add,
                 )
 
         def scores(g):
             b, h = divmod(g, H)
-            score[g] = work.tile([P, NB, T], F32, name="score")
+            in_sbuf = NB - blocks_added_by_tensor(g)
+            score[g] = []
+            rows = work.tile([P, in_sbuf, T], F32, tag="score")
+            top = work.tile([P, NB], F32)
             for j in range(NB):
-                ac = psum_score.tile([P, T], F32)
+                by_tensor = j >= in_sbuf
+                ac = psum_score.tile([P, T], F32, tag="sum" if by_tensor else "ac")
                 for e in range(2):
                     nc.tensor.matmul(
                         out=ac[:],
                         lhsT=qT[b][:, h, j * P : (j + 1) * P, e],
                         rhs=kT[b][:, h, :, e],
                         start=(e == 0),
-                        stop=(e == 1),
+                        stop=(e == 1 and not by_tensor),
                     )
-                nc.vector.tensor_tensor(
-                    out=score[g][:, j, :], in0=ac[:], in1=bd_rows[g][:, j, :], op=ALU.add
-                )
-            top = work.tile([P, NB], F32)
-            nc.vector.tensor_reduce(out=top[:], in_=score[g][:], axis=AXIS.X, op=ALU.max)
+                if by_tensor:
+                    nc.tensor.matmul(
+                        out=ac[:],
+                        lhsT=ident_bf16[:],
+                        rhs=bd_rows[g][:, j, :],
+                        start=False,
+                        stop=True,
+                    )
+                    nc.vector.tensor_reduce(
+                        out=top[:, j : j + 1], in_=ac[:], axis=AXIS.X, op=ALU.max
+                    )
+                    score[g].append(ac[:])
+                else:
+                    nc.vector.tensor_tensor(
+                        out=rows[:, j, :], in0=ac[:], in1=bd_rows[g][:, j, :], op=ALU.add
+                    )
+                    score[g].append(rows[:, j, :])
+            nc.vector.tensor_reduce(out=top[:, 0:in_sbuf], in_=rows[:], axis=AXIS.X, op=ALU.max)
             shift[g] = work.tile([P, NB], F32, name="shift")
             nc.vector.tensor_scalar_mul(out=shift[g][:], in0=top[:], scalar1=-SCALE)
 
@@ -151,7 +181,7 @@ def tile_attentionforonnx_pa_t_kernel(tc, q_u, k, matrix_bd, x, Wv, bv, out):
             for j in range(NB):
                 nc.scalar.activation(
                     out=e_rows[g][:, j, :],
-                    in_=score[g][:, j, :],
+                    in_=score[g][j],
                     func=ACT.Exp,
                     bias=shift[g][:, j : j + 1],
                     scale=SCALE,
@@ -178,12 +208,23 @@ def tile_attentionforonnx_pa_t_kernel(tc, q_u, k, matrix_bd, x, Wv, bv, out):
                         start=True,
                         stop=True,
                     )
-                nc.vector.tensor_tensor(
-                    out=o_rows[:, 2 * half : 2 * half + 2, :],
-                    in0=o_acc[:],
-                    in1=recip[g][:, 2 * half : 2 * half + 2].unsqueeze(2).to_broadcast([P, 2, HD]),
-                    op=ALU.mult,
-                )
+                if h == 1 and half == 0:
+                    pair = recip[g][:, 2 * half : 2 * half + 2]
+                    nc.vector.tensor_tensor(
+                        out=o_rows[:, 2 * half : 2 * half + 2, :],
+                        in0=o_acc[:],
+                        in1=pair.unsqueeze(2).to_broadcast([P, 2, HD]),
+                        op=ALU.mult,
+                    )
+                else:
+                    for i in range(2):
+                        j = 2 * half + i
+                        nc.scalar.activation(
+                            out=o_rows[:, j, :],
+                            in_=o_acc[:, i, :],
+                            func=ACT.Copy,
+                            scale=recip[g][:, j : j + 1],
+                        )
             nc.sync.dma_start(
                 out=out[b, :, h * HD : (h + 1) * HD].rearrange("(p j) c -> p j c", j=NB),
                 in_=o_rows[:],
@@ -195,15 +236,14 @@ def tile_attentionforonnx_pa_t_kernel(tc, q_u, k, matrix_bd, x, Wv, bv, out):
         w_rows = const.tile([P, NB, E], BF16)
         nc.sync.dma_start(out=w_rows[:], in_=Wv.rearrange("(f p) c -> p f c", p=P))
         load_x(0)
-        bv_rows = const.tile([P, P], BF16)
-        nc.vector.memset(bv_rows[:], 0.0)
-        nc.sync.dma_start(out=bv_rows[0:NB, :], in_=bv.rearrange("(f c) -> f c", c=P))
         load_bd(1)
         load_k(1)
         load_q(1)
         load_bd(2)
         load_bd(3)
         load_x(1)
+        bias_rows = const.tile([P, E], BF16)
+        nc.sync.dma_start(out=bias_rows[:], in_=bv.partition_broadcast(P))
 
         kT[0] = heads_to_partitions(k_rows[0][:], "kT")
         qT[0] = heads_to_partitions(q_rows[0][:], "qT")
@@ -216,22 +256,18 @@ def tile_attentionforonnx_pa_t_kernel(tc, q_u, k, matrix_bd, x, Wv, bv, out):
                 load_bd(H * (b + 2))
                 load_bd(H * (b + 2) + 1)
                 load_x(b + 2)
-            if step < GROUPS:
-                scores(step)
             if 0 <= step - 1 < GROUPS:
                 exponentials(step - 1)
+            if step < GROUPS:
+                scores(step)
             if not odd and 0 <= b - 1 < B:
-                v_mx[b - 1] = pack_for_mx(vT_rows[b - 1][:], "v", 2)
+                v_mx[b - 1] = quantize(v_grouped[b - 1][:].rearrange("p f t -> p (f t)"), "v", 2)
             if odd and b + 1 < B:
                 qT[b + 1] = heads_to_partitions(q_rows[b + 1][:], "qT")
             if 0 <= step - 1 < GROUPS:
                 e_mx[step - 1] = pack_for_mx(e_rows[step - 1][:], "e", OUTPUT_LAG)
             if step == 0:
                 w_codes, w_scales = pack_for_mx(w_rows[:], "w", 1)
-                bv_turned = psum_ring.tile([P, P], BF16, tag="ring")
-                nc.tensor.transpose(out=bv_turned[:], in_=bv_rows[:], identity=ident_bf16[:])
-                bias_col = const.tile([P, NB], F32)
-                nc.vector.tensor_copy(out=bias_col[:], in_=bv_turned[:, 0:NB])
             if not odd and b < B:
                 x_mx[b] = pack_for_mx(x_rows[b][:], "x", 2)
             if not odd and b + 1 < B:

@@ -18,15 +18,22 @@ P = 128
 NB = T // P
 REL = 2 * T - 1
 SCALE = 1.0 / 16.0
-GROUPS = B * H
-def blocks_added_by_tensor(g):
-    return 2 if g % 3 == 1 else 1
+HALVES = 2 * B * H
+SEQ = 2 * H
+ALL, FIRST, LAST = slice(0, NB), slice(0, NB // 2), slice(NB // 2, NB)
 
-
-OUTPUT_LAG = 2
+TURN_LAG, QUANTIZE_LAG, MIX_LAG, DIVIDE_LAG = 3, 4, 5, 6
 
 FLOPS = 3 * 2 * B * T * T * E
 BYTES = 2 * (3 * B * T * E + B * H * T * T + E * E + E) + 4 * B * T * E
+
+
+def added_by_tensor(p):
+    return p % 3 != 0
+
+
+def divided_by_vector(p):
+    return p >= HALVES - 4
 
 
 def tile_attentionforonnx_pa_t_kernel(tc, q_u, k, matrix_bd, x, Wv, bv, out):
@@ -34,68 +41,35 @@ def tile_attentionforonnx_pa_t_kernel(tc, q_u, k, matrix_bd, x, Wv, bv, out):
     with ExitStack() as stack:
         const = stack.enter_context(tc.tile_pool(name="const", bufs=1))
         io = stack.enter_context(tc.tile_pool(name="io", bufs=3))
-        work = stack.enter_context(tc.tile_pool(name="work", bufs=2))
-        psum_score = stack.enter_context(tc.psum_pool(name="psum_score", bufs=2))
-        psum_ring = stack.enter_context(tc.psum_pool(name="psum_ring", bufs=4))
+        work = stack.enter_context(tc.tile_pool(name="work", bufs=3))
+        psum = stack.enter_context(tc.psum_pool(name="psum", bufs=2))
 
         x_rows, k_rows, q_rows, bd_rows = {}, {}, {}, {}
-        x_mx, v_mx, e_mx = {}, {}, {}
-        v_grouped, qT, kT = {}, {}, {}
-        score, shift, e_rows, recip = {}, {}, {}, {}
+        ac, score, top, shift, e_rows, rowsum, recip = {}, {}, {}, {}, {}, {}, {}
+        e_grouped, e_mx, o_acc, o_rows = {}, {}, {}, {}
+        qT, kT = {}, {}
+        x_grouped, x_mx, v_acc, v_grouped, v_mx = {}, {}, {}, {}, {}
+        turned = {}
 
         ident_f32 = const.tile([P, P], F32)
         make_identity(nc, ident_f32[:])
-
         ident_bf16 = const.tile([P, P], BF16)
         nc.vector.tensor_copy(out=ident_bf16[:], in_=ident_f32[:])
 
-        def quantize(grouped, name, bufs):
-            codes = work.tile([P, NB * P], U32, tag=name + "_codes", bufs=bufs, align_bytes=64)
-            scales = work.tile([P, NB * P], U8, tag=name + "_scales", bufs=bufs, align_bytes=64)
-            nc.vector.quantize_mx(out=codes[:].bitcast(FP8X4), scales=scales[:], in_=grouped)
-            return codes, scales
-
-        def pack_for_mx(rows, name, bufs):
-            words = rows.bitcast(F32)
-            grouped = work.tile([P, NB * P * 4], BF16, tag="grouped", bufs=3, align_bytes=64)
-            grouped_words = grouped[:].bitcast(F32).rearrange("p (i r u) -> p i r u", i=NB, u=2)
-            for half in range(NB // 2):
-                turned = psum_ring.tile([P, 2, 2, P], F32, tag="ring")
-                for i in range(2):
-                    for u in range(2):
-                        nc.tensor.transpose(
-                            out=turned[:, i, u, :],
-                            in_=words[:, 2 * half + i, u * P : (u + 1) * P],
-                            identity=ident_f32[:],
-                        )
-                nc.scalar.copy(
-                    out=grouped_words[:, 2 * half : 2 * half + 2],
-                    in_=turned[:].rearrange("p i u r -> p i r u"),
-                )
-            return quantize(grouped[:], name, bufs)
-
-        def heads_to_partitions(rows, name):
-            words = rows.bitcast(F32)
-            turned_words = work.tile([P, H, NB, P], F32, tag=name)
-            for h in range(H):
-                turned = psum_ring.tile([P, NB, P], F32, tag="ring")
-                for i in range(NB):
-                    nc.tensor.transpose(
-                        out=turned[:, i, :],
-                        in_=words[:, i, h * P : (h + 1) * P],
-                        identity=ident_f32[:],
-                    )
-                nc.scalar.copy(out=turned_words[:, h], in_=turned[:])
-            return turned_words[:].bitcast(BF16).rearrange("p h i (r e) -> p h (i r) e", e=2)
-
-        def load_k(b):
-            k_rows[b] = io.tile([P, NB, E], BF16, name="k_rows")
-            nc.sync.dma_start(out=k_rows[b][:], in_=k[b].rearrange("(i p) h d -> p i (h d)", p=P))
-
-        def load_q(b):
-            q_rows[b] = io.tile([P, NB, E], BF16, name="q_rows")
+        def load_k(b, blocks=ALL):
+            if b not in k_rows:
+                k_rows[b] = io.tile([P, NB, E], BF16, name="k_rows")
             nc.sync.dma_start(
-                out=q_rows[b][:], in_=q_u[b].rearrange("(p j) h d -> p j (h d)", j=NB)
+                out=k_rows[b][:, blocks],
+                in_=k[b].rearrange("(i p) h d -> p i (h d)", p=P)[:, blocks],
+            )
+
+        def load_q(b, blocks=ALL):
+            if b not in q_rows:
+                q_rows[b] = io.tile([P, NB, E], BF16, name="q_rows")
+            nc.sync.dma_start(
+                out=q_rows[b][:, blocks],
+                in_=q_u[b].rearrange("(p j) h d -> p j (h d)", j=NB)[:, blocks],
             )
 
         def load_x(b):
@@ -105,134 +79,244 @@ def tile_attentionforonnx_pa_t_kernel(tc, q_u, k, matrix_bd, x, Wv, bv, out):
                 in_=x[b].rearrange("(u p e) c -> p u (e c)", u=2, e=2),
             )
 
-        def load_bd(g):
+        def load_bd(g, blocks=ALL):
             b, h = divmod(g, H)
             flat = matrix_bd[b, h].rearrange("t r -> (t r)")
             skewed = flat[T - 1 : T - 1 + T * (REL - 1)].rearrange(
                 "(p j c) -> p j c", j=NB, c=REL - 1
             )
-            bd_rows[g] = io.tile([P, NB, T], BF16, name="bd_rows", bufs=3 * H)
-            nc.sync.dma_start(out=bd_rows[g][:], in_=skewed[:, :, 0:T])
+            if g not in bd_rows:
+                bd_rows[g] = io.tile([P, NB, T], BF16, name="bd_rows", bufs=3 * H)
+            nc.sync.dma_start(out=bd_rows[g][:, blocks], in_=skewed[:, blocks, 0:T])
 
-        def project_v(b):
-            x_codes, x_scales = x_mx[b]
-            v_grouped[b] = work.tile([P, E, NB], BF16, name="v_grouped", align_bytes=64)
-            for f in range(NB):
-                features = slice(f * P, (f + 1) * P)
-                v_acc = psum_ring.tile([P, NB, P], F32, tag="ring")
-                for t in range(NB):
-                    nc.tensor.matmul_mx(
-                        out=v_acc[:, t, :],
-                        lhsT=x_codes[:, t * P : (t + 1) * P].bitcast(FP8X4),
-                        lhsT_scale=x_scales[:, t * P : (t + 1) * P],
-                        rhs=w_codes[:, features].bitcast(FP8X4),
-                        rhs_scale=w_scales[:, features],
-                        start=True,
-                        stop=True,
+        def copy_out(engine, out, in_):
+            if engine is nc.scalar:
+                nc.scalar.copy(out=out, in_=in_)
+            else:
+                nc.vector.tensor_copy(out=out, in_=in_)
+
+        def turn_words(key, rows2):
+            words = rows2.bitcast(F32)
+            bank = psum.tile([P, 2, 2, P], F32, tag="turned")
+            for i in range(2):
+                for u in range(2):
+                    nc.tensor.transpose(
+                        out=bank[:, i, u, :],
+                        in_=words[:, i, u * P : (u + 1) * P],
+                        identity=ident_f32[:],
                     )
-                nc.vector.tensor_tensor(
-                    out=v_grouped[b][:, features, :],
-                    in0=v_acc[:].rearrange("p t f -> p f t"),
-                    in1=bias_rows[:, features].unsqueeze(2).to_broadcast([P, P, NB]),
-                    op=ALU.add,
+            turned[key] = bank
+
+        def pack_words(key, engine, out):
+            copy_out(
+                engine,
+                out.bitcast(F32).rearrange("p (i r u) -> p i r u", i=2, u=2),
+                turned[key][:].rearrange("p i u r -> p i r u"),
+            )
+
+        def quantize(grouped, columns, name, bufs):
+            codes = work.tile([P, columns], U32, tag=name + "_codes", bufs=bufs, align_bytes=64)
+            scales = work.tile([P, columns], U8, tag=name + "_scales", bufs=bufs, align_bytes=64)
+            nc.vector.quantize_mx(out=codes[:].bitcast(FP8X4), scales=scales[:], in_=grouped)
+            return codes, scales
+
+        def turn_head(key, rows, h, blocks):
+            words = rows.bitcast(F32)
+            bank = psum.tile([P, NB, P], F32, tag="turned")
+            for i in range(blocks.start, blocks.stop):
+                nc.tensor.transpose(
+                    out=bank[:, i, :],
+                    in_=words[:, i, h * P : (h + 1) * P],
+                    identity=ident_f32[:],
+                )
+            turned[key] = bank
+
+        def keep_head(key, engine, kept, name, b, h, blocks):
+            if (b, h) not in kept:
+                kept[b, h] = work.tile([P, NB, P], F32, name=name, tag=name)
+            copy_out(engine, kept[b, h][:, blocks], turned[key][:, blocks])
+
+        def turn_job(job):
+            kind, b, i, blocks = job
+            if kind == "k":
+                turn_head(job, k_rows[b][:], i, blocks)
+            elif kind == "q":
+                turn_head(job, q_rows[b][:], i, blocks)
+            elif kind == "x":
+                turn_words(job, x_rows[b][:, blocks, :])
+            else:
+                turn_words(job, w_rows[:, blocks, :])
+
+        def copy_job(job, engine):
+            kind, b, i, blocks = job
+            if kind == "k":
+                keep_head(job, engine, kT, "kT", b, i, blocks)
+            elif kind == "q":
+                keep_head(job, engine, qT, "qT", b, i, blocks)
+            else:
+                if (kind, b) not in x_grouped:
+                    x_grouped[kind, b] = work.tile(
+                        [P, NB * P * 4], BF16, name="grouped", tag="grouped", bufs=3, align_bytes=64
+                    )
+                pack_words(
+                    job, engine, x_grouped[kind, b][:, blocks.start * 4 * P : blocks.stop * 4 * P]
                 )
 
-        def scores(g):
-            b, h = divmod(g, H)
-            in_sbuf = NB - blocks_added_by_tensor(g)
-            score[g] = []
-            rows = work.tile([P, in_sbuf, T], F32, tag="score")
-            top = work.tile([P, NB], F32)
-            for j in range(NB):
-                by_tensor = j >= in_sbuf
-                ac = psum_score.tile([P, T], F32, tag="sum" if by_tensor else "ac")
+        def pairs(tile):
+            return tile[:].bitcast(BF16).rearrange("p i (r e) -> p (i r) e", e=2)
+
+        def attend(p):
+            b, h, half = p // SEQ, p // 2 % H, p % 2
+            for i in range(2):
+                j = 2 * half + i
+                add = i == 1 and added_by_tensor(p)
+                bank = psum.tile([P, T], F32, tag="sum" if add else "ac")
                 for e in range(2):
                     nc.tensor.matmul(
-                        out=ac[:],
-                        lhsT=qT[b][:, h, j * P : (j + 1) * P, e],
-                        rhs=kT[b][:, h, :, e],
+                        out=bank[:],
+                        lhsT=pairs(qT[b, h])[:, j * P : (j + 1) * P, e],
+                        rhs=pairs(kT[b, h])[:, :, e],
                         start=(e == 0),
-                        stop=(e == 1 and not by_tensor),
+                        stop=(e == 1 and not add),
                     )
-                if by_tensor:
+                if add:
                     nc.tensor.matmul(
-                        out=ac[:],
+                        out=bank[:],
                         lhsT=ident_bf16[:],
-                        rhs=bd_rows[g][:, j, :],
+                        rhs=bd_rows[p // 2][:, j, :],
                         start=False,
                         stop=True,
                     )
-                    nc.vector.tensor_reduce(
-                        out=top[:, j : j + 1], in_=ac[:], axis=AXIS.X, op=ALU.max
-                    )
-                    score[g].append(ac[:])
-                else:
-                    nc.vector.tensor_tensor(
-                        out=rows[:, j, :], in0=ac[:], in1=bd_rows[g][:, j, :], op=ALU.add
-                    )
-                    score[g].append(rows[:, j, :])
-            nc.vector.tensor_reduce(out=top[:, 0:in_sbuf], in_=rows[:], axis=AXIS.X, op=ALU.max)
-            shift[g] = work.tile([P, NB], F32, name="shift")
-            nc.vector.tensor_scalar_mul(out=shift[g][:], in0=top[:], scalar1=-SCALE)
+                ac[p, i] = bank
 
-        def exponentials(g):
-            e_rows[g] = work.tile([P, NB, T], BF16, name="e_rows")
-            rowsum = work.tile([P, NB], F32)
-            for j in range(NB):
-                nc.scalar.activation(
-                    out=e_rows[g][:, j, :],
-                    in_=score[g][j],
-                    func=ACT.Exp,
-                    bias=shift[g][:, j : j + 1],
-                    scale=SCALE,
-                    accum_out=rowsum[:, j : j + 1],
-                )
-            recip[g] = work.tile([P, NB], F32, name="recip", bufs=OUTPUT_LAG + 1)
-            nc.vector.reciprocal(out=recip[g][:], in_=rowsum[:])
-
-        def output(g):
-            b, h = divmod(g, H)
-            e_codes, e_scales = e_mx[g]
-            v_codes, v_scales = v_mx[b]
-            o_rows = work.tile([P, NB, HD], F32, bufs=3)
-            for half in range(NB // 2):
-                o_acc = psum_ring.tile([P, 2, HD], F32, tag="ring")
-                for i in range(2):
-                    j = 2 * half + i
-                    nc.tensor.matmul_mx(
-                        out=o_acc[:, i, :],
-                        lhsT=e_codes[:, j * P : (j + 1) * P].bitcast(FP8X4),
-                        lhsT_scale=e_scales[:, j * P : (j + 1) * P],
-                        rhs=v_codes[:, h * HD : (h + 1) * HD].bitcast(FP8X4),
-                        rhs_scale=v_scales[:, h * HD : (h + 1) * HD],
-                        start=True,
-                        stop=True,
-                    )
-                if h == 1 and half == 0:
-                    pair = recip[g][:, 2 * half : 2 * half + 2]
-                    nc.vector.tensor_tensor(
-                        out=o_rows[:, 2 * half : 2 * half + 2, :],
-                        in0=o_acc[:],
-                        in1=pair.unsqueeze(2).to_broadcast([P, 2, HD]),
-                        op=ALU.mult,
-                    )
-                else:
-                    for i in range(2):
-                        j = 2 * half + i
-                        nc.scalar.activation(
-                            out=o_rows[:, j, :],
-                            in_=o_acc[:, i, :],
-                            func=ACT.Copy,
-                            scale=recip[g][:, j : j + 1],
-                        )
-            nc.sync.dma_start(
-                out=out[b, :, h * HD : (h + 1) * HD].rearrange("(p j) c -> p j c", j=NB),
-                in_=o_rows[:],
+        def set_shift(p, blocks):
+            nc.gpsimd.tensor_scalar(
+                out=shift[p][:, blocks],
+                in0=top[p][:, blocks],
+                scalar1=-SCALE,
+                scalar2=0.0,
+                op0=ALU.mult,
+                op1=ALU.add,
             )
 
-        load_k(0)
-        load_q(0)
-        load_bd(0)
+        def maximum_in_psum(p):
+            top[p] = work.tile([P, 2], F32, name="top", tag="top", bufs=4)
+            shift[p] = work.tile([P, 2], F32, name="shift", tag="shift", bufs=4)
+            if added_by_tensor(p):
+                nc.vector.tensor_reduce(
+                    out=top[p][:, 1:2], in_=ac[p, 1][:], axis=AXIS.X, op=ALU.max
+                )
+                set_shift(p, slice(1, 2))
+
+        def add_bd(p):
+            blocks = 1 if added_by_tensor(p) else 2
+            score[p] = work.tile([P, blocks, T], F32, name="score", tag="score")
+            for i in range(blocks):
+                nc.vector.tensor_tensor(
+                    out=score[p][:, i, :],
+                    in0=ac[p, i][:],
+                    in1=bd_rows[p // 2][:, 2 * (p % 2) + i, :],
+                    op=ALU.add,
+                )
+
+        def maximum_in_sbuf(p):
+            blocks = slice(0, 1 if added_by_tensor(p) else 2)
+            nc.vector.tensor_reduce(
+                out=top[p][:, blocks], in_=score[p][:], axis=AXIS.X, op=ALU.max
+            )
+            set_shift(p, blocks)
+
+        def exponential(p, i):
+            if p not in e_rows:
+                e_rows[p] = work.tile([P, 2, T], BF16, name="e_rows", tag="e_rows", bufs=4)
+                rowsum[p] = work.tile([P, 2], F32, name="rowsum", tag="rowsum", bufs=6)
+            nc.scalar.activation(
+                out=e_rows[p][:, i, :],
+                in_=ac[p, 1][:] if i == 1 and added_by_tensor(p) else score[p][:, i, :],
+                func=ACT.Exp,
+                bias=shift[p][:, i : i + 1],
+                scale=SCALE,
+                accum_out=rowsum[p][:, i : i + 1],
+            )
+
+        def pack_e(p, engine):
+            e_grouped[p] = work.tile([P, 2 * P * 4], BF16, name="e_grouped", tag="e_grouped", bufs=3, align_bytes=64)
+            pack_words(("e", p), engine, e_grouped[p][:])
+
+        def project(b, f):
+            x_codes, x_scales = x_mx[b]
+            w_codes, w_scales = x_mx["w"]
+            features = slice(f * P, (f + 1) * P)
+            v_acc[b, f] = psum.tile([P, NB, P], F32, name="product", tag="product")
+            for t in range(NB):
+                nc.tensor.matmul_mx(
+                    out=v_acc[b, f][:, t, :],
+                    lhsT=x_codes[:, t * P : (t + 1) * P].bitcast(FP8X4),
+                    lhsT_scale=x_scales[:, t * P : (t + 1) * P],
+                    rhs=w_codes[:, features].bitcast(FP8X4),
+                    rhs_scale=w_scales[:, features],
+                    start=True,
+                    stop=True,
+                )
+
+        def add_bias(b, f):
+            if f == 0:
+                v_grouped[b] = work.tile([P, E, NB], BF16, name="v_grouped", tag="v_grouped", bufs=2, align_bytes=64)
+            features = slice(f * P, (f + 1) * P)
+            nc.vector.tensor_tensor(
+                out=v_grouped[b][:, features, :],
+                in0=v_acc[b, f][:].rearrange("p t f -> p f t"),
+                in1=bias_rows[:, features].unsqueeze(2).to_broadcast([P, P, NB]),
+                op=ALU.add,
+            )
+
+        def mix_values(p):
+            b, h = p // SEQ, p // 2 % H
+            e_codes, e_scales = e_mx[p]
+            v_codes, v_scales = v_mx[b]
+            o_acc[p] = psum.tile([P, 2, HD], F32, name="product", tag="product")
+            for i in range(2):
+                nc.tensor.matmul_mx(
+                    out=o_acc[p][:, i, :],
+                    lhsT=e_codes[:, i * P : (i + 1) * P].bitcast(FP8X4),
+                    lhsT_scale=e_scales[:, i * P : (i + 1) * P],
+                    rhs=v_codes[:, h * HD : (h + 1) * HD].bitcast(FP8X4),
+                    rhs_scale=v_scales[:, h * HD : (h + 1) * HD],
+                    start=True,
+                    stop=True,
+                )
+
+        def divide(p):
+            b, h, half = p // SEQ, p // 2 % H, p % 2
+            rows = work.tile([P, 2, HD], F32, tag="o_rows")
+            if divided_by_vector(p):
+                nc.vector.tensor_tensor(
+                    out=rows[:],
+                    in0=o_acc[p][:],
+                    in1=recip[p][:].unsqueeze(2).to_broadcast([P, 2, HD]),
+                    op=ALU.mult,
+                )
+            else:
+                for i in range(2):
+                    nc.scalar.activation(
+                        out=rows[:, i, :],
+                        in_=o_acc[p][:, i, :],
+                        func=ACT.Copy,
+                        scale=recip[p][:, i : i + 1],
+                    )
+            nc.sync.dma_start(
+                out=out[b, :, h * HD : (h + 1) * HD].rearrange("(p j) c -> p j c", j=NB)[
+                    :, 2 * half : 2 * half + 2, :
+                ],
+                in_=rows[:],
+            )
+
+        load_q(0, FIRST)
+        load_k(0, FIRST)
+        load_k(0, LAST)
+        load_bd(0, FIRST)
+        load_q(0, LAST)
+        load_bd(0, LAST)
         w_rows = const.tile([P, NB, E], BF16)
         nc.sync.dma_start(out=w_rows[:], in_=Wv.rearrange("(f p) c -> p f c", p=P))
         load_x(0)
@@ -240,39 +324,99 @@ def tile_attentionforonnx_pa_t_kernel(tc, q_u, k, matrix_bd, x, Wv, bv, out):
         load_k(1)
         load_q(1)
         load_bd(2)
-        load_bd(3)
         load_x(1)
         bias_rows = const.tile([P, E], BF16)
         nc.sync.dma_start(out=bias_rows[:], in_=bv.partition_broadcast(P))
+        load_bd(3)
 
-        kT[0] = heads_to_partitions(k_rows[0][:], "kT")
-        qT[0] = heads_to_partitions(q_rows[0][:], "qT")
+        jobs = {p: [] for p in range(-1, HALVES + DIVIDE_LAG)}
+        for b in range(2, B):
+            jobs[SEQ * b - 3] += [(("k", b, 0, ALL), nc.scalar)]
+            jobs[SEQ * b - 2] += [(("q", b, 0, ALL), nc.scalar), (("x", b, 0, FIRST), nc.scalar)]
+            jobs[SEQ * b - 1] += [(("x", b, 0, LAST), nc.scalar)]
+            jobs[SEQ * b] += [(("k", b, 1, ALL), nc.scalar), (("q", b, 1, ALL), nc.scalar)]
+        first = [
+            (("q", 0, 0, FIRST), nc.vector),
+            (("k", 0, 0, FIRST), nc.scalar),
+            (("k", 0, 0, LAST), nc.vector),
+        ]
+        for job, engine in first:
+            turn_job(job)
+            copy_job(job, engine)
+        jobs[-1] = [(("q", 0, 0, LAST), nc.scalar)]
+        jobs[0] = [
+            (("k", 0, 1, ALL), nc.scalar),
+            (("q", 0, 1, ALL), nc.scalar),
+        ]
+        jobs[1] = [
+            (("w", 0, 0, FIRST), nc.scalar),
+            (("w", 0, 0, LAST), nc.scalar),
+            (("x", 0, 0, FIRST), nc.scalar),
+            (("x", 0, 0, LAST), nc.scalar),
+        ]
+        jobs[2] = [(("k", 1, 0, ALL), nc.scalar), (("q", 1, 0, ALL), nc.scalar)]
+        jobs[3] = [(("x", 1, 0, FIRST), nc.scalar), (("x", 1, 0, LAST), nc.scalar)]
+        jobs[4] = [(("k", 1, 1, ALL), nc.scalar), (("q", 1, 1, ALL), nc.scalar)]
+        chunks = {p: [] for p in range(-1, HALVES + DIVIDE_LAG)}
+        for b in range(B):
+            for f in range(NB):
+                chunks[SEQ * b + f if b else 2 + f // 2].append((b, f))
 
-        for step in range(GROUPS + OUTPUT_LAG):
-            b, odd = divmod(step, 2)
-            if not odd and b + 2 < B:
+        stack.enter_context(
+            tc.manual_schedule(
+                engines={mybir.EngineType.PE, mybir.EngineType.Activation, mybir.EngineType.DVE}
+            )
+        )
+        for p in range(-1, HALVES + DIVIDE_LAG):
+            b, r = divmod(p, SEQ)
+            if p >= 0 and r == 0 and b + 2 < B:
                 load_k(b + 2)
                 load_q(b + 2)
                 load_bd(H * (b + 2))
                 load_bd(H * (b + 2) + 1)
                 load_x(b + 2)
-            if 0 <= step - 1 < GROUPS:
-                exponentials(step - 1)
-            if step < GROUPS:
-                scores(step)
-            if not odd and 0 <= b - 1 < B:
-                v_mx[b - 1] = quantize(v_grouped[b - 1][:].rearrange("p f t -> p (f t)"), "v", 2)
-            if odd and b + 1 < B:
-                qT[b + 1] = heads_to_partitions(q_rows[b + 1][:], "qT")
-            if 0 <= step - 1 < GROUPS:
-                e_mx[step - 1] = pack_for_mx(e_rows[step - 1][:], "e", OUTPUT_LAG)
-            if step == 0:
-                w_codes, w_scales = pack_for_mx(w_rows[:], "w", 1)
-            if not odd and b < B:
-                x_mx[b] = pack_for_mx(x_rows[b][:], "x", 2)
-            if not odd and b + 1 < B:
-                kT[b + 1] = heads_to_partitions(k_rows[b + 1][:], "kT")
-            if odd and b < B:
-                project_v(b)
-            if 0 <= step - OUTPUT_LAG < GROUPS:
-                output(step - OUTPUT_LAG)
+            if 0 <= p < HALVES:
+                maximum_in_psum(p)
+            if 0 <= p < HALVES:
+                add_bd(p)
+            if 0 <= p - QUANTIZE_LAG < HALVES:
+                e_mx[p - QUANTIZE_LAG] = quantize(e_grouped[p - QUANTIZE_LAG][:], 2 * P, "e", 4)
+            for job in chunks.get(p - 1, []):
+                add_bias(*job)
+            if 0 <= p < HALVES:
+                maximum_in_sbuf(p)
+            if 0 <= p - TURN_LAG < HALVES:
+                turn_words(("e", p - TURN_LAG), e_rows[p - TURN_LAG][:])
+                pack_e(p - TURN_LAG, nc.scalar)
+            for job, engine in jobs[p][:1]:
+                turn_job(job)
+                copy_job(job, engine)
+            if p + 1 < HALVES:
+                attend(p + 1)
+            if 0 <= p - DIVIDE_LAG < HALVES:
+                divide(p - DIVIDE_LAG)
+            if 0 <= p - 1 < HALVES and not added_by_tensor(p - 1):
+                exponential(p - 1, 1)
+            if 0 <= p - 1 < HALVES:
+                exponential(p - 1, 0)
+            for job, engine in jobs[p][1:]:
+                turn_job(job)
+                copy_job(job, engine)
+            if 0 <= p < HALVES and added_by_tensor(p):
+                exponential(p, 1)
+            if p == 2:
+                x_mx["w"] = quantize(x_grouped["w", 0][:], NB * P, "w", 1)
+                x_mx[0] = quantize(x_grouped["x", 0][:], NB * P, "x", 2)
+            if r == 0 and 0 < b < B:
+                x_mx[b] = quantize(x_grouped["x", b][:], NB * P, "x", 2)
+            if r == 0 and 0 < b <= B:
+                v_mx[b - 1] = quantize(
+                    v_grouped[b - 1][:].rearrange("p f t -> p (f t)"), E, "v", 2
+                )
+            if 0 <= p - TURN_LAG < HALVES:
+                recip[p - TURN_LAG] = work.tile([P, 2], F32, name="recip", tag="recip", bufs=8)
+                nc.vector.reciprocal(out=recip[p - TURN_LAG][:], in_=rowsum[p - TURN_LAG][:])
+            for job in chunks[p]:
+                project(*job)
+            if 0 <= p - MIX_LAG < HALVES:
+                mix_values(p - MIX_LAG)

@@ -33,7 +33,7 @@ def added_by_tensor(p):
 
 
 def divided_by_vector(p):
-    return p >= HALVES - 4
+    return p >= HALVES - 6
 
 
 def tile_attentionforonnx_pa_t_kernel(tc, q_u, k, matrix_bd, x, Wv, bv, out):
@@ -97,7 +97,7 @@ def tile_attentionforonnx_pa_t_kernel(tc, q_u, k, matrix_bd, x, Wv, bv, out):
 
         def turn_words(key, rows2):
             words = rows2.bitcast(F32)
-            bank = psum.tile([P, 2, 2, P], F32, tag="turned")
+            bank = psum.tile([P, 2, 2, P], F32, tag="ring", bufs=4)
             for i in range(2):
                 for u in range(2):
                     nc.tensor.transpose(
@@ -122,7 +122,7 @@ def tile_attentionforonnx_pa_t_kernel(tc, q_u, k, matrix_bd, x, Wv, bv, out):
 
         def turn_head(key, rows, h, blocks):
             words = rows.bitcast(F32)
-            bank = psum.tile([P, NB, P], F32, tag="turned")
+            bank = psum.tile([P, NB, P], F32, tag="ring", bufs=4)
             for i in range(blocks.start, blocks.stop):
                 nc.tensor.transpose(
                     out=bank[:, i, :],
@@ -247,7 +247,7 @@ def tile_attentionforonnx_pa_t_kernel(tc, q_u, k, matrix_bd, x, Wv, bv, out):
             x_codes, x_scales = x_mx[b]
             w_codes, w_scales = x_mx["w"]
             features = slice(f * P, (f + 1) * P)
-            v_acc[b, f] = psum.tile([P, NB, P], F32, name="product", tag="product")
+            v_acc[b, f] = psum.tile([P, NB, P], F32, name="product", tag="ring", bufs=4)
             for t in range(NB):
                 nc.tensor.matmul_mx(
                     out=v_acc[b, f][:, t, :],
@@ -274,7 +274,7 @@ def tile_attentionforonnx_pa_t_kernel(tc, q_u, k, matrix_bd, x, Wv, bv, out):
             b, h = p // SEQ, p // 2 % H
             e_codes, e_scales = e_mx[p]
             v_codes, v_scales = v_mx[b]
-            o_acc[p] = psum.tile([P, 2, HD], F32, name="product", tag="product")
+            o_acc[p] = psum.tile([P, 2, HD], F32, name="product", tag="ring", bufs=4)
             for i in range(2):
                 nc.tensor.matmul_mx(
                     out=o_acc[p][:, i, :],
@@ -379,12 +379,16 @@ def tile_attentionforonnx_pa_t_kernel(tc, q_u, k, matrix_bd, x, Wv, bv, out):
                 maximum_in_psum(p)
             if 0 <= p < HALVES:
                 add_bd(p)
-            if 0 <= p - QUANTIZE_LAG < HALVES:
-                e_mx[p - QUANTIZE_LAG] = quantize(e_grouped[p - QUANTIZE_LAG][:], 2 * P, "e", 4)
             for job in chunks.get(p - 1, []):
                 add_bias(*job)
             if 0 <= p < HALVES:
                 maximum_in_sbuf(p)
+            if 0 <= p - QUANTIZE_LAG < HALVES:
+                e_mx[p - QUANTIZE_LAG] = quantize(e_grouped[p - QUANTIZE_LAG][:], 2 * P, "e", 4)
+            if 0 <= p - DIVIDE_LAG < HALVES:
+                divide(p - DIVIDE_LAG)
+            if 0 <= p - 1 < HALVES and not added_by_tensor(p - 1):
+                exponential(p - 1, 1)
             if 0 <= p - TURN_LAG < HALVES:
                 turn_words(("e", p - TURN_LAG), e_rows[p - TURN_LAG][:])
                 pack_e(p - TURN_LAG, nc.scalar)
@@ -393,10 +397,6 @@ def tile_attentionforonnx_pa_t_kernel(tc, q_u, k, matrix_bd, x, Wv, bv, out):
                 copy_job(job, engine)
             if p + 1 < HALVES:
                 attend(p + 1)
-            if 0 <= p - DIVIDE_LAG < HALVES:
-                divide(p - DIVIDE_LAG)
-            if 0 <= p - 1 < HALVES and not added_by_tensor(p - 1):
-                exponential(p - 1, 1)
             if 0 <= p - 1 < HALVES:
                 exponential(p - 1, 0)
             for job, engine in jobs[p][1:]:

@@ -33,7 +33,7 @@ def added_by_tensor(p):
 
 
 def divided_by_vector(p):
-    return p >= HALVES - 6
+    return p >= HALVES - 4
 
 
 def tile_attentionforonnx_pa_t_kernel(tc, q_u, k, matrix_bd, x, Wv, bv, out):
@@ -227,16 +227,18 @@ def tile_attentionforonnx_pa_t_kernel(tc, q_u, k, matrix_bd, x, Wv, bv, out):
             set_shift(p, blocks)
 
         def exponential(p, i):
+            g, half = divmod(p, 2)
             if p not in e_rows:
                 e_rows[p] = work.tile([P, 2, T], BF16, name="e_rows", tag="e_rows", bufs=4)
-                rowsum[p] = work.tile([P, 2], F32, name="rowsum", tag="rowsum", bufs=6)
+            if g not in rowsum:
+                rowsum[g] = work.tile([P, NB], F32, name="rowsum", tag="rowsum", bufs=4)
             nc.scalar.activation(
                 out=e_rows[p][:, i, :],
                 in_=ac[p, 1][:] if i == 1 and added_by_tensor(p) else score[p][:, i, :],
                 func=ACT.Exp,
                 bias=shift[p][:, i : i + 1],
                 scale=SCALE,
-                accum_out=rowsum[p][:, i : i + 1],
+                accum_out=rowsum[g][:, 2 * half + i : 2 * half + i + 1],
             )
 
         def pack_e(p, engine):
@@ -293,7 +295,7 @@ def tile_attentionforonnx_pa_t_kernel(tc, q_u, k, matrix_bd, x, Wv, bv, out):
                 nc.vector.tensor_tensor(
                     out=rows[:],
                     in0=o_acc[p][:],
-                    in1=recip[p][:].unsqueeze(2).to_broadcast([P, 2, HD]),
+                    in1=recip[p // 2][:, 2 * half : 2 * half + 2].unsqueeze(2).to_broadcast([P, 2, HD]),
                     op=ALU.mult,
                 )
             else:
@@ -302,7 +304,7 @@ def tile_attentionforonnx_pa_t_kernel(tc, q_u, k, matrix_bd, x, Wv, bv, out):
                         out=rows[:, i, :],
                         in_=o_acc[p][:, i, :],
                         func=ACT.Copy,
-                        scale=recip[p][:, i : i + 1],
+                        scale=recip[p // 2][:, 2 * half + i : 2 * half + i + 1],
                     )
             nc.sync.dma_start(
                 out=out[b, :, h * HD : (h + 1) * HD].rearrange("(p j) c -> p j c", j=NB)[
@@ -376,17 +378,17 @@ def tile_attentionforonnx_pa_t_kernel(tc, q_u, k, matrix_bd, x, Wv, bv, out):
                 load_bd(H * (b + 2) + 1)
                 load_x(b + 2)
             if 0 <= p < HALVES:
-                maximum_in_psum(p)
-            if 0 <= p < HALVES:
                 add_bd(p)
+            if 0 <= p < HALVES:
+                maximum_in_psum(p)
             for job in chunks.get(p - 1, []):
                 add_bias(*job)
             if 0 <= p < HALVES:
                 maximum_in_sbuf(p)
-            if 0 <= p - QUANTIZE_LAG < HALVES:
-                e_mx[p - QUANTIZE_LAG] = quantize(e_grouped[p - QUANTIZE_LAG][:], 2 * P, "e", 4)
             if 0 <= p - DIVIDE_LAG < HALVES:
                 divide(p - DIVIDE_LAG)
+            if 0 <= p - QUANTIZE_LAG < HALVES:
+                e_mx[p - QUANTIZE_LAG] = quantize(e_grouped[p - QUANTIZE_LAG][:], 2 * P, "e", 4)
             if 0 <= p - 1 < HALVES and not added_by_tensor(p - 1):
                 exponential(p - 1, 1)
             if 0 <= p - TURN_LAG < HALVES:
@@ -395,15 +397,17 @@ def tile_attentionforonnx_pa_t_kernel(tc, q_u, k, matrix_bd, x, Wv, bv, out):
             for job, engine in jobs[p][:1]:
                 turn_job(job)
                 copy_job(job, engine)
+            for job, engine in jobs[p][1:]:
+                turn_job(job)
+                copy_job(job, engine)
             if p + 1 < HALVES:
                 attend(p + 1)
             if 0 <= p - 1 < HALVES:
                 exponential(p - 1, 0)
-            for job, engine in jobs[p][1:]:
-                turn_job(job)
-                copy_job(job, engine)
             if 0 <= p < HALVES and added_by_tensor(p):
                 exponential(p, 1)
+            if 0 <= p - MIX_LAG < HALVES:
+                mix_values(p - MIX_LAG)
             if p == 2:
                 x_mx["w"] = quantize(x_grouped["w", 0][:], NB * P, "w", 1)
                 x_mx[0] = quantize(x_grouped["x", 0][:], NB * P, "x", 2)
@@ -413,10 +417,9 @@ def tile_attentionforonnx_pa_t_kernel(tc, q_u, k, matrix_bd, x, Wv, bv, out):
                 v_mx[b - 1] = quantize(
                     v_grouped[b - 1][:].rearrange("p f t -> p (f t)"), E, "v", 2
                 )
-            if 0 <= p - TURN_LAG < HALVES:
-                recip[p - TURN_LAG] = work.tile([P, 2], F32, name="recip", tag="recip", bufs=8)
-                nc.vector.reciprocal(out=recip[p - TURN_LAG][:], in_=rowsum[p - TURN_LAG][:])
+            if 0 <= p - TURN_LAG < HALVES and p % 2 == 0:
+                g = (p - TURN_LAG) // 2
+                recip[g] = work.tile([P, NB], F32, name="recip", tag="recip", bufs=4)
+                nc.vector.reciprocal(out=recip[g][:], in_=rowsum[g][:])
             for job in chunks[p]:
                 project(*job)
-            if 0 <= p - MIX_LAG < HALVES:
-                mix_values(p - MIX_LAG)

@@ -162,6 +162,21 @@ def tile_attentionforonnx_pa_t_kernel(tc, q_u, k, matrix_bd, x, Wv, bv, out):
                     job, engine, x_grouped[kind, b][:, blocks.start * 4 * P : blocks.stop * 4 * P]
                 )
 
+        def turn_bias():
+            bank = psum.tile([P, P], BF16, name="ring", tag="ring", bufs=4)
+            nc.tensor.transpose(out=bank[:], in_=bv_rows[:], identity=ident_bf16[:])
+            nc.scalar.copy(out=bv_columns[:], in_=bank[:, 0:NB])
+
+        def spread_bias():
+            bank = psum.tile([P, NB, P], BF16, name="ring", tag="ring", bufs=4)
+            for f in range(NB):
+                nc.tensor.transpose(
+                    out=bank[:, f, :],
+                    in_=bv_columns[:, f : f + 1].to_broadcast([P, P]),
+                    identity=ident_bf16[:],
+                )
+            nc.scalar.copy(out=bias_rows[:], in_=bank[:].rearrange("p f c -> p (f c)"))
+
         def pairs(tile):
             return tile[:].bitcast(BF16).rearrange("p i (r e) -> p (i r) e", e=2)
 
@@ -322,13 +337,16 @@ def tile_attentionforonnx_pa_t_kernel(tc, q_u, k, matrix_bd, x, Wv, bv, out):
         w_rows = const.tile([P, NB, E], BF16)
         nc.sync.dma_start(out=w_rows[:], in_=Wv.rearrange("(f p) c -> p f c", p=P))
         load_x(0)
+        bv_rows = const.tile([P, P], BF16)
+        nc.vector.memset(bv_rows[:], 0.0)
+        nc.sync.dma_start(out=bv_rows[0:NB, :], in_=bv.rearrange("(f c) -> f c", c=P))
+        bv_columns = const.tile([P, NB], BF16)
+        bias_rows = const.tile([P, E], BF16)
         load_bd(1)
         load_k(1)
         load_q(1)
         load_bd(2)
         load_x(1)
-        bias_rows = const.tile([P, E], BF16)
-        nc.sync.dma_start(out=bias_rows[:], in_=bv.partition_broadcast(P))
         load_bd(3)
 
         jobs = {p: [] for p in range(-1, HALVES + DIVIDE_LAG)}
@@ -400,6 +418,10 @@ def tile_attentionforonnx_pa_t_kernel(tc, q_u, k, matrix_bd, x, Wv, bv, out):
             for job, engine in jobs[p][1:]:
                 turn_job(job)
                 copy_job(job, engine)
+            if p == 1:
+                turn_bias()
+            if p == 2:
+                spread_bias()
             if p + 1 < HALVES:
                 attend(p + 1)
             if 0 <= p - 1 < HALVES:

@@ -20,6 +20,7 @@ REL = 2 * T - 1
 SCALE = 1.0 / 16.0
 HALVES = 2 * B * H
 SEQ = 2 * H
+WARM_UP = 12
 ALL, FIRST, LAST = slice(0, NB), slice(0, NB // 2), slice(NB // 2, NB)
 
 TURN_LAG, QUANTIZE_LAG, MIX_LAG, DIVIDE_LAG = 3, 4, 5, 6
@@ -33,7 +34,7 @@ def added_by_tensor(p):
 
 
 def divided_by_vector(p):
-    return p >= HALVES - 4
+    return p >= HALVES - 4 and p % 2 == 0
 
 
 def tile_attentionforonnx_pa_t_kernel(tc, q_u, k, matrix_bd, x, Wv, bv, out):
@@ -355,6 +356,16 @@ def tile_attentionforonnx_pa_t_kernel(tc, q_u, k, matrix_bd, x, Wv, bv, out):
             jobs[SEQ * b - 2] += [(("q", b, 0, ALL), nc.scalar), (("x", b, 0, FIRST), nc.scalar)]
             jobs[SEQ * b - 1] += [(("x", b, 0, LAST), nc.scalar)]
             jobs[SEQ * b] += [(("k", b, 1, ALL), nc.scalar), (("q", b, 1, ALL), nc.scalar)]
+        stack.enter_context(
+            tc.manual_schedule(
+                engines={mybir.EngineType.PE, mybir.EngineType.Activation, mybir.EngineType.DVE}
+            )
+        )
+        bank = psum.tile([P, NB, P], F32, name="ring", tag="ring", bufs=4)
+        for i in range(WARM_UP):
+            nc.tensor.transpose(
+                out=bank[:, i % NB, :], in_=ident_f32[:], identity=ident_f32[:]
+            )
         first = [
             (("q", 0, 0, FIRST), nc.vector),
             (("k", 0, 0, FIRST), nc.scalar),
@@ -382,11 +393,6 @@ def tile_attentionforonnx_pa_t_kernel(tc, q_u, k, matrix_bd, x, Wv, bv, out):
             for f in range(NB):
                 chunks[SEQ * b + f if b else 2 + f // 2].append((b, f))
 
-        stack.enter_context(
-            tc.manual_schedule(
-                engines={mybir.EngineType.PE, mybir.EngineType.Activation, mybir.EngineType.DVE}
-            )
-        )
         for p in range(-1, HALVES + DIVIDE_LAG):
             b, r = divmod(p, SEQ)
             if p >= 0 and r == 0 and b + 2 < B:
@@ -418,16 +424,16 @@ def tile_attentionforonnx_pa_t_kernel(tc, q_u, k, matrix_bd, x, Wv, bv, out):
             for job, engine in jobs[p][1:]:
                 turn_job(job)
                 copy_job(job, engine)
-            if p == 1:
-                turn_bias()
-            if p == 2:
-                spread_bias()
             if p + 1 < HALVES:
                 attend(p + 1)
             if 0 <= p - 1 < HALVES:
                 exponential(p - 1, 0)
             if 0 <= p < HALVES and added_by_tensor(p):
                 exponential(p, 1)
+            if p == 0:
+                turn_bias()
+            if p == 1:
+                spread_bias()
             if 0 <= p - MIX_LAG < HALVES:
                 mix_values(p - MIX_LAG)
             if p == 2:

@@ -421,13 +421,13 @@ def tile_attentionforonnx_pa_t_kernel(tc, q_u, k, matrix_bd, x, Wv, bv, out):
             for job, engine in jobs[p][:1]:
                 turn_job(job)
                 copy_job(job, engine)
-            for job, engine in jobs[p][1:]:
-                turn_job(job)
-                copy_job(job, engine)
             if p + 1 < HALVES:
                 attend(p + 1)
             if 0 <= p - 1 < HALVES:
                 exponential(p - 1, 0)
+            for job, engine in jobs[p][1:]:
+                turn_job(job)
+                copy_job(job, engine)
             if 0 <= p < HALVES and added_by_tensor(p):
                 exponential(p, 1)
             if p == 0:

@@ -306,7 +306,7 @@ def tile_attentionforonnx_pa_t_kernel(tc, q_u, k, matrix_bd, x, Wv, bv, out):
 
         def divide(p):
             b, h, half = p // SEQ, p // 2 % H, p % 2
-            rows = work.tile([P, 2, HD], F32, tag="o_rows")
+            rows = work.tile([P, 2, HD], F32, tag="o_rows", bufs=6)
             if divided_by_vector(p):
                 nc.vector.tensor_tensor(
                     out=rows[:],
@@ -395,12 +395,16 @@ def tile_attentionforonnx_pa_t_kernel(tc, q_u, k, matrix_bd, x, Wv, bv, out):
 
         for p in range(-1, HALVES + DIVIDE_LAG):
             b, r = divmod(p, SEQ)
-            if p >= 0 and r == 0 and b + 2 < B:
-                load_k(b + 2)
-                load_q(b + 2)
-                load_bd(H * (b + 2))
-                load_bd(H * (b + 2) + 1)
-                load_x(b + 2)
+            if p >= 0 and b + 2 < B:
+                if r == 0:
+                    load_k(b + 2)
+                elif r == 1:
+                    load_q(b + 2)
+                    load_bd(H * (b + 2))
+                elif r == 2:
+                    load_bd(H * (b + 2) + 1)
+                else:
+                    load_x(b + 2)
             if 0 <= p < HALVES:
                 add_bd(p)
             if 0 <= p < HALVES:

@@ -181,29 +181,28 @@ def tile_attentionforonnx_pa_t_kernel(tc, q_u, k, matrix_bd, x, Wv, bv, out):
         def pairs(tile):
             return tile[:].bitcast(BF16).rearrange("p i (r e) -> p (i r) e", e=2)
 
-        def attend(p):
+        def attend(p, i):
             b, h, half = p // SEQ, p // 2 % H, p % 2
-            for i in range(2):
-                j = 2 * half + i
-                add = i == 1 and added_by_tensor(p)
-                bank = psum.tile([P, T], F32, tag="sum" if add else "ac")
-                for e in range(2):
-                    nc.tensor.matmul(
-                        out=bank[:],
-                        lhsT=pairs(qT[b, h])[:, j * P : (j + 1) * P, e],
-                        rhs=pairs(kT[b, h])[:, :, e],
-                        start=(e == 0),
-                        stop=(e == 1 and not add),
-                    )
-                if add:
-                    nc.tensor.matmul(
-                        out=bank[:],
-                        lhsT=ident_bf16[:],
-                        rhs=bd_rows[p // 2][:, j, :],
-                        start=False,
-                        stop=True,
-                    )
-                ac[p, i] = bank
+            j = 2 * half + i
+            add = i == 1 and added_by_tensor(p)
+            bank = psum.tile([P, T], F32, tag="sum" if add else "ac")
+            for e in range(2):
+                nc.tensor.matmul(
+                    out=bank[:],
+                    lhsT=pairs(qT[b, h])[:, j * P : (j + 1) * P, e],
+                    rhs=pairs(kT[b, h])[:, :, e],
+                    start=(e == 0),
+                    stop=(e == 1 and not add),
+                )
+            if add:
+                nc.tensor.matmul(
+                    out=bank[:],
+                    lhsT=ident_bf16[:],
+                    rhs=bd_rows[p // 2][:, j, :],
+                    start=False,
+                    stop=True,
+                )
+            ac[p, i] = bank
 
         def set_shift(p, blocks):
             nc.gpsimd.tensor_scalar(
@@ -378,16 +377,25 @@ def tile_attentionforonnx_pa_t_kernel(tc, q_u, k, matrix_bd, x, Wv, bv, out):
         jobs[0] = [
             (("k", 0, 1, ALL), nc.scalar),
             (("q", 0, 1, ALL), nc.scalar),
+            (("w", 0, 0, FIRST), nc.scalar),
         ]
         jobs[1] = [
-            (("w", 0, 0, FIRST), nc.scalar),
             (("w", 0, 0, LAST), nc.scalar),
             (("x", 0, 0, FIRST), nc.scalar),
             (("x", 0, 0, LAST), nc.scalar),
         ]
-        jobs[2] = [(("k", 1, 0, ALL), nc.scalar), (("q", 1, 0, ALL), nc.scalar)]
-        jobs[3] = [(("x", 1, 0, FIRST), nc.scalar), (("x", 1, 0, LAST), nc.scalar)]
-        jobs[4] = [(("k", 1, 1, ALL), nc.scalar), (("q", 1, 1, ALL), nc.scalar)]
+        jobs[2] = [
+            (("k", 1, 0, ALL), nc.scalar),
+            (("q", 1, 0, ALL), nc.scalar),
+        ]
+        jobs[3] = [
+            (("x", 1, 0, FIRST), nc.scalar),
+            (("x", 1, 0, LAST), nc.scalar),
+        ]
+        jobs[4] = [
+            (("k", 1, 1, ALL), nc.scalar),
+            (("q", 1, 1, ALL), nc.scalar),
+        ]
         chunks = {p: [] for p in range(-1, HALVES + DIVIDE_LAG)}
         for b in range(B):
             for f in range(NB):
@@ -426,12 +434,14 @@ def tile_attentionforonnx_pa_t_kernel(tc, q_u, k, matrix_bd, x, Wv, bv, out):
                 turn_job(job)
                 copy_job(job, engine)
             if p + 1 < HALVES:
-                attend(p + 1)
-            if 0 <= p - 1 < HALVES:
-                exponential(p - 1, 0)
+                attend(p + 1, 0)
             for job, engine in jobs[p][1:]:
                 turn_job(job)
                 copy_job(job, engine)
+            if p + 1 < HALVES:
+                attend(p + 1, 1)
+            if 0 <= p - 1 < HALVES:
+                exponential(p - 1, 0)
             if 0 <= p < HALVES and added_by_tensor(p):
                 exponential(p, 1)
             if p == 0:

@@ -33,8 +33,15 @@ def added_by_tensor(p):
     return p % 3 != 0
 
 
+def due(p, lag):
+    n = p - lag
+    if n == HALVES - 2:
+        return [n, n + 1]
+    return [n] if 0 <= n < HALVES - 2 else []
+
+
 def divided_by_vector(p):
-    return p >= HALVES - 4 and p % 2 == 0
+    return p >= HALVES - 6 and p % 2 == 1
 
 
 def tile_attentionforonnx_pa_t_kernel(tc, q_u, k, matrix_bd, x, Wv, bv, out):
@@ -60,9 +67,9 @@ def tile_attentionforonnx_pa_t_kernel(tc, q_u, k, matrix_bd, x, Wv, bv, out):
         def load_k(b, blocks=ALL):
             if b not in k_rows:
                 k_rows[b] = io.tile([P, NB, E], BF16, name="k_rows")
+            order = "(i p) h d -> p i (h d)" if b == 0 else "(p i) h d -> p i (h d)"
             nc.sync.dma_start(
-                out=k_rows[b][:, blocks],
-                in_=k[b].rearrange("(i p) h d -> p i (h d)", p=P)[:, blocks],
+                out=k_rows[b][:, blocks], in_=k[b].rearrange(order, p=P)[:, blocks]
             )
 
         def load_q(b, blocks=ALL):
@@ -135,7 +142,12 @@ def tile_attentionforonnx_pa_t_kernel(tc, q_u, k, matrix_bd, x, Wv, bv, out):
         def keep_head(key, engine, kept, name, b, h, blocks):
             if (b, h) not in kept:
                 kept[b, h] = work.tile([P, NB, P], F32, name=name, tag=name)
-            copy_out(engine, kept[b, h][:, blocks], turned[key][:, blocks])
+            source = turned[key][:, blocks]
+            target = kept[b, h][:, blocks]
+            if name == "kT" and b > 0:
+                source = source.rearrange("p i r -> p r i")
+                target = target.rearrange("p i r -> p (i r)").rearrange("p (r i) -> p r i", i=NB)
+            copy_out(engine, target, source)
 
         def turn_job(job):
             kind, b, i, blocks = job
@@ -257,7 +269,7 @@ def tile_attentionforonnx_pa_t_kernel(tc, q_u, k, matrix_bd, x, Wv, bv, out):
             )
 
         def pack_e(p, engine):
-            e_grouped[p] = work.tile([P, 2 * P * 4], BF16, name="e_grouped", tag="e_grouped", bufs=3, align_bytes=64)
+            e_grouped[p] = work.tile([P, 2 * P * 4], BF16, name="e_grouped", tag="e_grouped", bufs=4, align_bytes=64)
             pack_words(("e", p), engine, e_grouped[p][:])
 
         def project(b, f):
@@ -349,7 +361,7 @@ def tile_attentionforonnx_pa_t_kernel(tc, q_u, k, matrix_bd, x, Wv, bv, out):
         load_x(1)
         load_bd(3)
 
-        jobs = {p: [] for p in range(-1, HALVES + DIVIDE_LAG)}
+        jobs = {p: [] for p in range(-1, HALVES - 1 + DIVIDE_LAG)}
         for b in range(2, B):
             jobs[SEQ * b - 3] += [(("k", b, 0, ALL), nc.scalar)]
             jobs[SEQ * b - 2] += [(("q", b, 0, ALL), nc.scalar), (("x", b, 0, FIRST), nc.scalar)]
@@ -396,12 +408,12 @@ def tile_attentionforonnx_pa_t_kernel(tc, q_u, k, matrix_bd, x, Wv, bv, out):
             (("k", 1, 1, ALL), nc.scalar),
             (("q", 1, 1, ALL), nc.scalar),
         ]
-        chunks = {p: [] for p in range(-1, HALVES + DIVIDE_LAG)}
+        chunks = {p: [] for p in range(-1, HALVES - 1 + DIVIDE_LAG)}
         for b in range(B):
             for f in range(NB):
                 chunks[SEQ * b + f if b else 2 + f // 2].append((b, f))
 
-        for p in range(-1, HALVES + DIVIDE_LAG):
+        for p in range(-1, HALVES - 1 + DIVIDE_LAG):
             b, r = divmod(p, SEQ)
             if p >= 0 and b + 2 < B:
                 if r == 0:
@@ -421,15 +433,15 @@ def tile_attentionforonnx_pa_t_kernel(tc, q_u, k, matrix_bd, x, Wv, bv, out):
                 add_bias(*job)
             if 0 <= p < HALVES:
                 maximum_in_sbuf(p)
-            if 0 <= p - DIVIDE_LAG < HALVES:
-                divide(p - DIVIDE_LAG)
-            if 0 <= p - QUANTIZE_LAG < HALVES:
-                e_mx[p - QUANTIZE_LAG] = quantize(e_grouped[p - QUANTIZE_LAG][:], 2 * P, "e", 4)
+            for n in due(p, DIVIDE_LAG):
+                divide(n)
+            for n in due(p, QUANTIZE_LAG):
+                e_mx[n] = quantize(e_grouped[n][:], 2 * P, "e", 4)
             if 0 <= p - 1 < HALVES and not added_by_tensor(p - 1):
                 exponential(p - 1, 1)
-            if 0 <= p - TURN_LAG < HALVES:
-                turn_words(("e", p - TURN_LAG), e_rows[p - TURN_LAG][:])
-                pack_e(p - TURN_LAG, nc.scalar)
+            for n in due(p, TURN_LAG):
+                turn_words(("e", n), e_rows[n][:])
+                pack_e(n, nc.scalar)
             for job, engine in jobs[p][:1]:
                 turn_job(job)
                 copy_job(job, engine)
@@ -448,8 +460,8 @@ def tile_attentionforonnx_pa_t_kernel(tc, q_u, k, matrix_bd, x, Wv, bv, out):
                 turn_bias()
             if p == 1:
                 spread_bias()
-            if 0 <= p - MIX_LAG < HALVES:
-                mix_values(p - MIX_LAG)
+            for n in due(p, MIX_LAG):
+                mix_values(n)
             if p == 2:
                 x_mx["w"] = quantize(x_grouped["w", 0][:], NB * P, "w", 1)
                 x_mx[0] = quantize(x_grouped["x", 0][:], NB * P, "x", 2)
@@ -459,9 +471,9 @@ def tile_attentionforonnx_pa_t_kernel(tc, q_u, k, matrix_bd, x, Wv, bv, out):
                 v_mx[b - 1] = quantize(
                     v_grouped[b - 1][:].rearrange("p f t -> p (f t)"), E, "v", 2
                 )
-            if 0 <= p - TURN_LAG < HALVES and p % 2 == 0:
-                g = (p - TURN_LAG) // 2
-                recip[g] = work.tile([P, NB], F32, name="recip", tag="recip", bufs=4)
-                nc.vector.reciprocal(out=recip[g][:], in_=rowsum[g][:])
+            for n in due(p, TURN_LAG):
+                if n % 2 == 1:
+                    recip[n // 2] = work.tile([P, NB], F32, name="recip", tag="recip", bufs=4)
+                    nc.vector.reciprocal(out=recip[n // 2][:], in_=rowsum[n // 2][:])
             for job in chunks[p]:
                 project(*job)

from contextlib import ExitStack

import concourse.mybir as mybir
from concourse.masks import make_identity

F32 = mybir.dt.float32
BF16 = mybir.dt.bfloat16
U32 = mybir.dt.uint32
U8 = mybir.dt.uint8
FP8X4 = mybir.dt.float8_e4m3fn_x4
ALU = mybir.AluOpType
ACT = mybir.ActivationFunctionType
AXIS = mybir.AxisListType

B, T, E, H = 8, 512, 512, 2
HD = E // H
P = 128
NB = T // P
REL = 2 * T - 1
SCALE = 1.0 / 16.0
HALVES = 2 * B * H
SEQ = 2 * H
WARM_UP = 12
ALL, FIRST, LAST = slice(0, NB), slice(0, NB // 2), slice(NB // 2, NB)

TURN_LAG, QUANTIZE_LAG, MIX_LAG, DIVIDE_LAG = 3, 4, 5, 6

FLOPS = 3 * 2 * B * T * T * E
BYTES = 2 * (3 * B * T * E + B * H * T * T + E * E + E) + 4 * B * T * E


def added_by_tensor(p):
    return p % 3 != 0


def due(p, lag):
    n = p - lag
    if n == HALVES - 2:
        return [n, n + 1]
    return [n] if 0 <= n < HALVES - 2 else []


def divided_by_vector(p):
    return p >= HALVES - 6 and p % 2 == 1


def tile_attentionforonnx_pa_t_kernel(tc, q_u, k, matrix_bd, x, Wv, bv, out):
    nc = tc.nc
    with ExitStack() as stack:
        const = stack.enter_context(tc.tile_pool(name="const", bufs=1))
        io = stack.enter_context(tc.tile_pool(name="io", bufs=3))
        work = stack.enter_context(tc.tile_pool(name="work", bufs=3))
        psum = stack.enter_context(tc.psum_pool(name="psum", bufs=2))

        x_rows, k_rows, q_rows, bd_rows = {}, {}, {}, {}
        ac, score, top, shift, e_rows, rowsum, recip = {}, {}, {}, {}, {}, {}, {}
        e_grouped, e_mx, o_acc, o_rows = {}, {}, {}, {}
        qT, kT = {}, {}
        x_grouped, x_mx, v_acc, v_grouped, v_mx = {}, {}, {}, {}, {}
        turned = {}

        ident_f32 = const.tile([P, P], F32)
        make_identity(nc, ident_f32[:])
        ident_bf16 = const.tile([P, P], BF16)
        nc.vector.tensor_copy(out=ident_bf16[:], in_=ident_f32[:])

        def load_k(b, blocks=ALL):
            if b not in k_rows:
                k_rows[b] = io.tile([P, NB, E], BF16, name="k_rows")
            order = "(i p) h d -> p i (h d)" if b == 0 else "(p i) h d -> p i (h d)"
            nc.sync.dma_start(
                out=k_rows[b][:, blocks], in_=k[b].rearrange(order, p=P)[:, blocks]
            )

        def load_q(b, blocks=ALL):
            if b not in q_rows:
                q_rows[b] = io.tile([P, NB, E], BF16, name="q_rows")
            nc.sync.dma_start(
                out=q_rows[b][:, blocks],
                in_=q_u[b].rearrange("(p j) h d -> p j (h d)", j=NB)[:, blocks],
            )

        def load_x(b):
            x_rows[b] = io.tile([P, NB, E], BF16, name="x_rows")
            nc.sync.dma_start(
                out=x_rows[b][:].rearrange("p (u e) c -> p u (e c)", u=2),
                in_=x[b].rearrange("(u p e) c -> p u (e c)", u=2, e=2),
            )

        def load_bd(g, blocks=ALL):
            b, h = divmod(g, H)
            flat = matrix_bd[b, h].rearrange("t r -> (t r)")
            skewed = flat[T - 1 : T - 1 + T * (REL - 1)].rearrange(
                "(p j c) -> p j c", j=NB, c=REL - 1
            )
            if g not in bd_rows:
                bd_rows[g] = io.tile([P, NB, T], BF16, name="bd_rows", bufs=3 * H)
            nc.sync.dma_start(out=bd_rows[g][:, blocks], in_=skewed[:, blocks, 0:T])

        def copy_out(engine, out, in_):
            if engine is nc.scalar:
                nc.scalar.copy(out=out, in_=in_)
            else:
                nc.vector.tensor_copy(out=out, in_=in_)

        def turn_words(key, rows2):
            words = rows2.bitcast(F32)
            bank = psum.tile([P, 2, 2, P], F32, tag="ring", bufs=4)
            for i in range(2):
                for u in range(2):
                    nc.tensor.transpose(
                        out=bank[:, i, u, :],
                        in_=words[:, i, u * P : (u + 1) * P],
                        identity=ident_f32[:],
                    )
            turned[key] = bank

        def pack_words(key, engine, out):
            copy_out(
                engine,
                out.bitcast(F32).rearrange("p (i r u) -> p i r u", i=2, u=2),
                turned[key][:].rearrange("p i u r -> p i r u"),
            )

        def quantize(grouped, columns, name, bufs):
            codes = work.tile([P, columns], U32, tag=name + "_codes", bufs=bufs, align_bytes=64)
            scales = work.tile([P, columns], U8, tag=name + "_scales", bufs=bufs, align_bytes=64)
            nc.vector.quantize_mx(out=codes[:].bitcast(FP8X4), scales=scales[:], in_=grouped)
            return codes, scales

        def turn_head(key, rows, h, blocks):
            words = rows.bitcast(F32)
            bank = psum.tile([P, NB, P], F32, tag="ring", bufs=4)
            for i in range(blocks.start, blocks.stop):
                nc.tensor.transpose(
                    out=bank[:, i, :],
                    in_=words[:, i, h * P : (h + 1) * P],
                    identity=ident_f32[:],
                )
            turned[key] = bank

        def keep_head(key, engine, kept, name, b, h, blocks):
            if (b, h) not in kept:
                kept[b, h] = work.tile([P, NB, P], F32, name=name, tag=name)
            source = turned[key][:, blocks]
            target = kept[b, h][:, blocks]
            if name == "kT" and b > 0:
                source = source.rearrange("p i r -> p r i")
                target = target.rearrange("p i r -> p (i r)").rearrange("p (r i) -> p r i", i=NB)
            copy_out(engine, target, source)

        def turn_job(job):
            kind, b, i, blocks = job
            if kind == "k":
                turn_head(job, k_rows[b][:], i, blocks)
            elif kind == "q":
                turn_head(job, q_rows[b][:], i, blocks)
            elif kind == "x":
                turn_words(job, x_rows[b][:, blocks, :])
            else:
                turn_words(job, w_rows[:, blocks, :])

        def copy_job(job, engine):
            kind, b, i, blocks = job
            if kind == "k":
                keep_head(job, engine, kT, "kT", b, i, blocks)
            elif kind == "q":
                keep_head(job, engine, qT, "qT", b, i, blocks)
            else:
                if (kind, b) not in x_grouped:
                    x_grouped[kind, b] = work.tile(
                        [P, NB * P * 4], BF16, name="grouped", tag="grouped", bufs=3, align_bytes=64
                    )
                pack_words(
                    job, engine, x_grouped[kind, b][:, blocks.start * 4 * P : blocks.stop * 4 * P]
                )

        def turn_bias():
            bank = psum.tile([P, P], BF16, name="ring", tag="ring", bufs=4)
            nc.tensor.transpose(out=bank[:], in_=bv_rows[:], identity=ident_bf16[:])
            nc.scalar.copy(out=bv_columns[:], in_=bank[:, 0:NB])

        def spread_bias():
            bank = psum.tile([P, NB, P], BF16, name="ring", tag="ring", bufs=4)
            for f in range(NB):
                nc.tensor.transpose(
                    out=bank[:, f, :],
                    in_=bv_columns[:, f : f + 1].to_broadcast([P, P]),
                    identity=ident_bf16[:],
                )
            nc.scalar.copy(out=bias_rows[:], in_=bank[:].rearrange("p f c -> p (f c)"))

        def pairs(tile):
            return tile[:].bitcast(BF16).rearrange("p i (r e) -> p (i r) e", e=2)

        def attend(p, i):
            b, h, half = p // SEQ, p // 2 % H, p % 2
            j = 2 * half + i
            add = i == 1 and added_by_tensor(p)
            bank = psum.tile([P, T], F32, tag="sum" if add else "ac")
            for e in range(2):
                nc.tensor.matmul(
                    out=bank[:],
                    lhsT=pairs(qT[b, h])[:, j * P : (j + 1) * P, e],
                    rhs=pairs(kT[b, h])[:, :, e],
                    start=(e == 0),
                    stop=(e == 1 and not add),
                )
            if add:
                nc.tensor.matmul(
                    out=bank[:],
                    lhsT=ident_bf16[:],
                    rhs=bd_rows[p // 2][:, j, :],
                    start=False,
                    stop=True,
                )
            ac[p, i] = bank

        def set_shift(p, blocks):
            nc.gpsimd.tensor_scalar(
                out=shift[p][:, blocks],
                in0=top[p][:, blocks],
                scalar1=-SCALE,
                scalar2=0.0,
                op0=ALU.mult,
                op1=ALU.add,
            )

        def maximum_in_psum(p):
            top[p] = work.tile([P, 2], F32, name="top", tag="top", bufs=4)
            shift[p] = work.tile([P, 2], F32, name="shift", tag="shift", bufs=4)
            if added_by_tensor(p):
                nc.vector.tensor_reduce(
                    out=top[p][:, 1:2], in_=ac[p, 1][:], axis=AXIS.X, op=ALU.max
                )
                set_shift(p, slice(1, 2))

        def add_bd(p):
            blocks = 1 if added_by_tensor(p) else 2
            score[p] = work.tile([P, blocks, T], F32, name="score", tag="score")
            for i in range(blocks):
                nc.vector.tensor_tensor(
                    out=score[p][:, i, :],
                    in0=ac[p, i][:],
                    in1=bd_rows[p // 2][:, 2 * (p % 2) + i, :],
                    op=ALU.add,
                )

        def maximum_in_sbuf(p):
            blocks = slice(0, 1 if added_by_tensor(p) else 2)
            nc.vector.tensor_reduce(
                out=top[p][:, blocks], in_=score[p][:], axis=AXIS.X, op=ALU.max
            )
            set_shift(p, blocks)

        def exponential(p, i):
            g, half = divmod(p, 2)
            if p not in e_rows:
                e_rows[p] = work.tile([P, 2, T], BF16, name="e_rows", tag="e_rows", bufs=4)
            if g not in rowsum:
                rowsum[g] = work.tile([P, NB], F32, name="rowsum", tag="rowsum", bufs=4)
            nc.scalar.activation(
                out=e_rows[p][:, i, :],
                in_=ac[p, 1][:] if i == 1 and added_by_tensor(p) else score[p][:, i, :],
                func=ACT.Exp,
                bias=shift[p][:, i : i + 1],
                scale=SCALE,
                accum_out=rowsum[g][:, 2 * half + i : 2 * half + i + 1],
            )

        def pack_e(p, engine):
            e_grouped[p] = work.tile([P, 2 * P * 4], BF16, name="e_grouped", tag="e_grouped", bufs=4, align_bytes=64)
            pack_words(("e", p), engine, e_grouped[p][:])

        def project(b, f):
            x_codes, x_scales = x_mx[b]
            w_codes, w_scales = x_mx["w"]
            features = slice(f * P, (f + 1) * P)
            v_acc[b, f] = psum.tile([P, NB, P], F32, name="product", tag="ring", bufs=4)
            for t in range(NB):
                nc.tensor.matmul_mx(
                    out=v_acc[b, f][:, t, :],
                    lhsT=x_codes[:, t * P : (t + 1) * P].bitcast(FP8X4),
                    lhsT_scale=x_scales[:, t * P : (t + 1) * P],
                    rhs=w_codes[:, features].bitcast(FP8X4),
                    rhs_scale=w_scales[:, features],
                    start=True,
                    stop=True,
                )

        def add_bias(b, f):
            if f == 0:
                v_grouped[b] = work.tile([P, E, NB], BF16, name="v_grouped", tag="v_grouped", bufs=2, align_bytes=64)
            features = slice(f * P, (f + 1) * P)
            nc.vector.tensor_tensor(
                out=v_grouped[b][:, features, :],
                in0=v_acc[b, f][:].rearrange("p t f -> p f t"),
                in1=bias_rows[:, features].unsqueeze(2).to_broadcast([P, P, NB]),
                op=ALU.add,
            )

        def mix_values(p):
            b, h = p // SEQ, p // 2 % H
            e_codes, e_scales = e_mx[p]
            v_codes, v_scales = v_mx[b]
            o_acc[p] = psum.tile([P, 2, HD], F32, name="product", tag="ring", bufs=4)
            for i in range(2):
                nc.tensor.matmul_mx(
                    out=o_acc[p][:, i, :],
                    lhsT=e_codes[:, i * P : (i + 1) * P].bitcast(FP8X4),
                    lhsT_scale=e_scales[:, i * P : (i + 1) * P],
                    rhs=v_codes[:, h * HD : (h + 1) * HD].bitcast(FP8X4),
                    rhs_scale=v_scales[:, h * HD : (h + 1) * HD],
                    start=True,
                    stop=True,
                )

        def divide(p):
            b, h, half = p // SEQ, p // 2 % H, p % 2
            rows = work.tile([P, 2, HD], F32, tag="o_rows", bufs=6)
            if divided_by_vector(p):
                nc.vector.tensor_tensor(
                    out=rows[:],
                    in0=o_acc[p][:],
                    in1=recip[p // 2][:, 2 * half : 2 * half + 2].unsqueeze(2).to_broadcast([P, 2, HD]),
                    op=ALU.mult,
                )
            else:
                for i in range(2):
                    nc.scalar.activation(
                        out=rows[:, i, :],
                        in_=o_acc[p][:, i, :],
                        func=ACT.Copy,
                        scale=recip[p // 2][:, 2 * half + i : 2 * half + i + 1],
                    )
            nc.sync.dma_start(
                out=out[b, :, h * HD : (h + 1) * HD].rearrange("(p j) c -> p j c", j=NB)[
                    :, 2 * half : 2 * half + 2, :
                ],
                in_=rows[:],
            )

        load_q(0, FIRST)
        load_k(0, FIRST)
        load_k(0, LAST)
        load_bd(0, FIRST)
        load_q(0, LAST)
        load_bd(0, LAST)
        w_rows = const.tile([P, NB, E], BF16)
        nc.sync.dma_start(out=w_rows[:], in_=Wv.rearrange("(f p) c -> p f c", p=P))
        load_x(0)
        bv_rows = const.tile([P, P], BF16)
        nc.vector.memset(bv_rows[:], 0.0)
        nc.sync.dma_start(out=bv_rows[0:NB, :], in_=bv.rearrange("(f c) -> f c", c=P))
        bv_columns = const.tile([P, NB], BF16)
        bias_rows = const.tile([P, E], BF16)
        load_bd(1)
        load_k(1)
        load_q(1)
        load_bd(2)
        load_x(1)
        load_bd(3)

        jobs = {p: [] for p in range(-1, HALVES - 1 + DIVIDE_LAG)}
        for b in range(2, B):
            jobs[SEQ * b - 3] += [(("k", b, 0, ALL), nc.scalar)]
            jobs[SEQ * b - 2] += [(("q", b, 0, ALL), nc.scalar), (("x", b, 0, FIRST), nc.scalar)]
            jobs[SEQ * b - 1] += [(("x", b, 0, LAST), nc.scalar)]
            jobs[SEQ * b] += [(("k", b, 1, ALL), nc.scalar), (("q", b, 1, ALL), nc.scalar)]
        stack.enter_context(
            tc.manual_schedule(
                engines={mybir.EngineType.PE, mybir.EngineType.Activation, mybir.EngineType.DVE}
            )
        )
        bank = psum.tile([P, NB, P], F32, name="ring", tag="ring", bufs=4)
        for i in range(WARM_UP):
            nc.tensor.transpose(
                out=bank[:, i % NB, :], in_=ident_f32[:], identity=ident_f32[:]
            )
        first = [
            (("q", 0, 0, FIRST), nc.vector),
            (("k", 0, 0, FIRST), nc.scalar),
            (("k", 0, 0, LAST), nc.vector),
        ]
        for job, engine in first:
            turn_job(job)
            copy_job(job, engine)
        jobs[-1] = [(("q", 0, 0, LAST), nc.scalar)]
        jobs[0] = [
            (("k", 0, 1, ALL), nc.scalar),
            (("q", 0, 1, ALL), nc.scalar),
            (("w", 0, 0, FIRST), nc.scalar),
        ]
        jobs[1] = [
            (("w", 0, 0, LAST), nc.scalar),
            (("x", 0, 0, FIRST), nc.scalar),
            (("x", 0, 0, LAST), nc.scalar),
        ]
        jobs[2] = [
            (("k", 1, 0, ALL), nc.scalar),
            (("q", 1, 0, ALL), nc.scalar),
        ]
        jobs[3] = [
            (("x", 1, 0, FIRST), nc.scalar),
            (("x", 1, 0, LAST), nc.scalar),
        ]
        jobs[4] = [
            (("k", 1, 1, ALL), nc.scalar),
            (("q", 1, 1, ALL), nc.scalar),
        ]
        chunks = {p: [] for p in range(-1, HALVES - 1 + DIVIDE_LAG)}
        for b in range(B):
            for f in range(NB):
                chunks[SEQ * b + f if b else 2 + f // 2].append((b, f))

        for p in range(-1, HALVES - 1 + DIVIDE_LAG):
            b, r = divmod(p, SEQ)
            if p >= 0 and b + 2 < B:
                if r == 0:
                    load_k(b + 2)
                elif r == 1:
                    load_q(b + 2)
                    load_bd(H * (b + 2))
                elif r == 2:
                    load_bd(H * (b + 2) + 1)
                else:
                    load_x(b + 2)
            if 0 <= p < HALVES:
                add_bd(p)
            if 0 <= p < HALVES:
                maximum_in_psum(p)
            for job in chunks.get(p - 1, []):
                add_bias(*job)
            if 0 <= p < HALVES:
                maximum_in_sbuf(p)
            for n in due(p, DIVIDE_LAG):
                divide(n)
            for n in due(p, QUANTIZE_LAG):
                e_mx[n] = quantize(e_grouped[n][:], 2 * P, "e", 4)
            if 0 <= p - 1 < HALVES and not added_by_tensor(p - 1):
                exponential(p - 1, 1)
            for n in due(p, TURN_LAG):
                turn_words(("e", n), e_rows[n][:])
                pack_e(n, nc.scalar)
            for job, engine in jobs[p][:1]:
                turn_job(job)
                copy_job(job, engine)
            if p + 1 < HALVES:
                attend(p + 1, 0)
            for job, engine in jobs[p][1:]:
                turn_job(job)
                copy_job(job, engine)
            if p + 1 < HALVES:
                attend(p + 1, 1)
            if 0 <= p - 1 < HALVES:
                exponential(p - 1, 0)
            if 0 <= p < HALVES and added_by_tensor(p):
                exponential(p, 1)
            if p == 0:
                turn_bias()
            if p == 1:
                spread_bias()
            for n in due(p, MIX_LAG):
                mix_values(n)
            if p == 2:
                x_mx["w"] = quantize(x_grouped["w", 0][:], NB * P, "w", 1)
                x_mx[0] = quantize(x_grouped["x", 0][:], NB * P, "x", 2)
            if r == 0 and 0 < b < B:
                x_mx[b] = quantize(x_grouped["x", b][:], NB * P, "x", 2)
            if r == 0 and 0 < b <= B:
                v_mx[b - 1] = quantize(
                    v_grouped[b - 1][:].rearrange("p f t -> p (f t)"), E, "v", 2
                )
            for n in due(p, TURN_LAG):
                if n % 2 == 1:
                    recip[n // 2] = work.tile([P, NB], F32, name="recip", tag="recip", bufs=4)
                    nc.vector.reciprocal(out=recip[n // 2][:], in_=rowsum[n // 2][:])
            for job in chunks[p]:
                project(*job)
